import numpy as np
import ml_dtypes


def mxq(x, axis, fmt="e4m3"):
    dtype, down = {"e4m3": (ml_dtypes.float8_e4m3fn, 7), "e5m2": (ml_dtypes.float8_e5m2, 14)}[fmt]
    v = np.moveaxis(np.asarray(x, np.float32).astype(ml_dtypes.bfloat16).astype(np.float64), axis, -1)
    blocks = v.reshape(v.shape[:-1] + (-1, 32))
    amax = np.abs(blocks).max(-1, keepdims=True)
    byte = np.maximum(np.where(amax > 0, np.frexp(amax)[1] - 1 + 127, 0) - down, 1)
    scale = np.exp2(byte - 127.0)
    codes = (blocks / scale).astype(np.float32).astype(dtype).astype(np.float64)
    return np.moveaxis((codes * scale).reshape(v.shape), -1, axis)


WIDE = False


def mx_kscale(k):
    if not WIDE:
        return np.ones(k)
    levels = np.array([10, -10, 5, -5, 0])
    a = np.random.permutation(np.resize(levels, k // 512 * 4)).reshape(k // 512, 4)
    idx = np.arange(k)
    return np.exp2(a[idx // 512, idx % 128 // 32])


BF16 = ml_dtypes.bfloat16


def bf(x):
    return np.asarray(x, np.float32).astype(BF16)


def f64(x):
    return np.asarray(x).astype(np.float64)


H, W, B, D, N, L = 64, 64, 200, 512, 1024, 3
NEG_SLOPE = 0.01
EDGE_P = 0.05
EDGE_W = 0.25


def lrelu(v):
    return np.where(v > 0, v, NEG_SLOPE * v)


def setup_inputs():
    t = mx_kscale(D)
    a = (np.random.uniform(size=(N, N)) < EDGE_P) * np.random.uniform(size=(N, N)) * EDGE_W
    return {
        "h": bf(0.75 * np.random.standard_normal((N, D))),
        "adj": bf(np.maximum(a, a.T)),
        "gcn_bn_g": bf((1.0 + 0.1 * np.random.standard_normal(D)) * t),
        "gcn_bn_b": bf(0.1 * np.random.standard_normal(D) * t),
        "gcn_w": bf(np.random.standard_normal((D, D)) * 2.0 / np.sqrt(D) / t[:, None]),
        "gcn_b": bf(0.1 * np.random.standard_normal(D) - 0.1),
    }


def reference(h, adj, gcn_bn_g, gcn_bn_b, gcn_w, gcn_b):
    g = f64(adj) + np.eye(N)
    dinv = np.sum(g, axis=1) ** -0.5
    gn = dinv[:, None] * g * dinv[None, :]
    hb = f64(gcn_bn_g) * f64(h) + f64(gcn_bn_b)
    agg = mxq(gn, 1, "e4m3") @ mxq(hb, 0, "e4m3")
    return lrelu((mxq(agg, 1, "e4m3") @ mxq(f64(gcn_w), 0, "e4m3")) + f64(gcn_b))

@@ -1,0 +1,317 @@
+from contextlib import ExitStack
+
+from concourse import mybir
+from concourse.masks import make_identity
+
+BF16 = mybir.dt.bfloat16
+F32 = mybir.dt.float32
+U32 = mybir.dt.uint32
+U8 = mybir.dt.uint8
+FP8X4 = mybir.dt.float8_e4m3fn_x4
+ALU = mybir.AluOpType
+ACT = mybir.ActivationFunctionType
+
+P = 128
+N = 1024
+D = 512
+NT = N // P
+CT = D // P
+G = 2
+T = 4
+NEG_SLOPE = 0.01
+
+FLOPS = 2 * N * N * D + 2 * N * D * D
+
+
+def dinv_col(b):
+    return 4 * (b // 4) + 2 * (b % 2) + (b % 4) // 2
+
+
+def tile_tls_msc_pb_kernel(tc, h, adj, gcn_bn_g, gcn_bn_b, gcn_w, gcn_b, out):
+    nc = tc.nc
+    with ExitStack() as ctx:
+        keep = ctx.enter_context(tc.tile_pool(name="keep", bufs=1))
+        work = ctx.enter_context(tc.tile_pool(name="work", bufs=3))
+        ps_c = ctx.enter_context(tc.psum_pool(name="ps_c", bufs=1))
+        ps = ctx.enter_context(tc.psum_pool(name="ps", bufs=6))
+        ctx.enter_context(tc.manual_schedule())
+
+        ident_bf = keep.tile([P, P], BF16, name="ident_bf")
+        ident_f = keep.tile([P, P], F32, name="ident_f")
+        vecs = keep.tile([P, P], BF16, name="vecs")
+        warm = keep.tile([P, 1], F32, name="warm")
+        adj_sb = keep.tile([P, NT, N], BF16, name="adj_sb")
+        h_sb = keep.tile([P, NT, D], BF16, name="h_sb")
+        w_sb = keep.tile([P, T, D], BF16, name="w_sb")
+        bias_bc = keep.tile([P, D], BF16, name="bias_bc")
+        deg_v = keep.tile([P, 4], F32, name="deg_v")
+        deg_s = keep.tile([P, 4], F32, name="deg_s")
+        junk = keep.tile([P, N], BF16, name="junk")
+        gd = keep.tile([P, NT, P], F32, name="gd")
+        root = keep.tile([P, NT], F32, name="root")
+        dinv = keep.tile([P, NT], F32, name="dinv")
+        gb = keep.tile([P, 2 * CT], F32, name="gb")
+        hbt = keep.tile([P, CT, NT, P], BF16, name="hbt")
+        hb_g = keep.tile([P, G, D, T], BF16, name="hb_g", align_bytes=64)
+        hb_q = keep.tile([P, G, D], U32, name="hb_q", align_bytes=64)
+        hb_s = keep.tile([P, G, D], U8, name="hb_s", align_bytes=64)
+        w_g = keep.tile([P, D, T], BF16, name="w_g", align_bytes=64)
+        w_q = keep.tile([P, D], U32, name="w_q", align_bytes=64)
+        w_s = keep.tile([P, D], U8, name="w_s", align_bytes=64)
+        gn = keep.tile([P, NT, N], BF16, name="gn")
+        gn_q = keep.tile([P, NT, G, P], U32, name="gn_q", align_bytes=64)
+        gn_s = keep.tile([P, NT, G, P], U8, name="gn_s", align_bytes=64)
+        dbc = [ps_c.tile([P, 512], F32, name="dbc%d" % i) for i in range(2)]
+        live = {}
+
+        def setup():
+            make_identity(nc, ident_bf[:])
+            make_identity(nc, ident_f[:])
+            nc.vector.memset(vecs[:], 0.0)
+            nc.vector.memset(warm[:], 1.0)
+            nc.scalar.activation(out=warm[:], in_=warm[:], func=ACT.Sqrt)
+            nc.scalar.dma_start(out=vecs[0:CT, :], in_=gcn_bn_g.rearrange("(t p) -> t p", p=P))
+            nc.scalar.dma_start(out=vecs[CT : 2 * CT, :], in_=gcn_bn_b.rearrange("(t p) -> t p", p=P))
+            for b in range(NT):
+                nc.sync.dma_start(out=adj_sb[:, b, :], in_=adj[b * P : (b + 1) * P, :])
+            h_v = h.rearrange("(a p) c -> p a c", p=P)
+            nc.sync.dma_start(out=h_sb[:, 0:4, :], in_=h_v[:, 0:4, :])
+            nc.sync.dma_start(out=h_sb[:, 4:8, :], in_=h_v[:, 4:8, :])
+            nc.sync.dma_start(out=w_sb[:], in_=gcn_w.rearrange("(t p) d -> p t d", p=P))
+            nc.sync.dma_start(out=bias_bc[:], in_=gcn_b.partition_broadcast(P))
+
+        def vec_columns():
+            tv = ps.tile([P, NT, P], BF16, name="tv", tag="ps")
+            nc.tensor.transpose(out=tv[:, 0, :], in_=vecs[:], identity=ident_bf[:])
+            nc.vector.tensor_copy(out=gb[:], in_=tv[:, 0, 0 : 2 * CT])
+
+        def row_sum(b):
+            k = b // 2
+            if b % 2 == 0:
+                nc.vector.tensor_reduce(
+                    out=deg_v[:, k : k + 1], in_=adj_sb[:, b, :], axis=mybir.AxisListType.X, op=ALU.add
+                )
+            else:
+                nc.scalar.activation(
+                    out=junk[:], in_=adj_sb[:, b, :], func=ACT.Copy, accum_out=deg_s[:, k : k + 1]
+                )
+            nc.gpsimd.tensor_tensor(
+                out=gd[:, b, :], in0=adj_sb[:, b, b * P : (b + 1) * P], in1=ident_f[:], op=ALU.add
+            )
+
+        def roots(q):
+            nc.scalar.activation(
+                out=root[:, 4 * q : 4 * q + 2], in_=deg_v[:, 2 * q : 2 * q + 2], func=ACT.Sqrt, bias=1.0
+            )
+            nc.scalar.activation(
+                out=root[:, 4 * q + 2 : 4 * q + 4], in_=deg_s[:, 2 * q : 2 * q + 2], func=ACT.Sqrt, bias=1.0
+            )
+
+        def recip(q):
+            nc.vector.reciprocal(out=dinv[:, 4 * q : 4 * q + 4], in_=root[:, 4 * q : 4 * q + 4])
+
+        def spread(q):
+            for r in range(4):
+                c = dinv_col(4 * q + r)
+                nc.tensor.transpose(
+                    out=dbc[q][:, r * P : (r + 1) * P],
+                    in_=dinv[:, c : c + 1].to_broadcast([P, P]),
+                    identity=ident_f[:],
+                )
+
+        def scale(b, half):
+            c = dinv_col(b)
+            cuts = sorted(set([512 * half, 512 * half + 512] + [x for x in (b * P, (b + 1) * P) if x // 512 == half]))
+            for lo, hi in zip(cuts[:-1], cuts[1:]):
+                src = gd[:, b, :] if lo == b * P else adj_sb[:, b, lo:hi]
+                nc.vector.scalar_tensor_tensor(
+                    out=gn[:, b, lo:hi],
+                    in0=src,
+                    scalar=dinv[:, c : c + 1],
+                    in1=dbc[half][:, lo - 512 * half : hi - 512 * half],
+                    op0=ALU.mult,
+                    op1=ALU.mult,
+                )
+
+        def h_turn(ct, half):
+            t1 = ps.tile([P, 4, P], BF16, name="t1", tag="ps")
+            for a in range(4):
+                nc.tensor.transpose(
+                    out=t1[:, a, :], in_=h_sb[:, 4 * half + a, ct * P : (ct + 1) * P], identity=ident_bf[:]
+                )
+            live["t1", ct, half] = t1
+
+        def h_affine(ct, half):
+            nc.scalar.activation(
+                out=hbt[:, ct, 4 * half : 4 * half + 4, :],
+                in_=live["t1", ct, half][:],
+                func=ACT.Identity,
+                scale=gb[:, ct : ct + 1],
+                bias=gb[:, CT + ct : CT + ct + 1],
+            )
+
+        def hb_turn(ct):
+            t2 = ps.tile([P, NT, P], BF16, name="t2", tag="ps")
+            for a in range(NT):
+                nc.tensor.transpose(out=t2[:, a, :], in_=hbt[:, ct, a, :], identity=ident_bf[:])
+            live["t2", ct] = t2
+
+        def hb_group(ct):
+            nc.scalar.copy(
+                out=hb_g[:, :, ct * P : (ct + 1) * P, :],
+                in_=live["t2", ct][:].rearrange("p (g t) c -> p g c t", g=G),
+            )
+
+        def hb_quant(g):
+            nc.vector.quantize_mx(
+                out=hb_q[:, g, :].bitcast(FP8X4),
+                scales=hb_s[:, g, :],
+                in_=hb_g[:, g, :, :].rearrange("p c t -> p (c t)"),
+            )
+
+        def w_group():
+            nc.gpsimd.tensor_scalar(
+                out=w_g[:], in0=w_sb[:].rearrange("p t d -> p d t"), scalar1=1.0, scalar2=0.0, op0=ALU.mult, op1=ALU.add
+            )
+
+        def w_quant():
+            nc.vector.quantize_mx(
+                out=w_q[:].bitcast(FP8X4), scales=w_s[:], in_=w_g[:].rearrange("p d t -> p (d t)")
+            )
+
+        def gn_turn(b):
+            t3 = ps.tile([P, NT, P], BF16, name="t3", tag="ps")
+            for a in range(NT):
+                nc.tensor.transpose(out=t3[:, a, :], in_=gn[:, b, a * P : (a + 1) * P], identity=ident_bf[:])
+            live["t3", b] = t3
+
+        def gn_group(b):
+            gn_g = work.tile([P, G, P, T], BF16, name="gn_g", align_bytes=64)
+            nc.scalar.copy(out=gn_g[:], in_=live["t3", b][:].rearrange("p (g t) i -> p g i t", g=G))
+            live["gn_g", b] = gn_g
+
+        def gn_quant(b):
+            nc.vector.quantize_mx(
+                out=gn_q[:, b, :, :].rearrange("p g i -> p (g i)").bitcast(FP8X4),
+                scales=gn_s[:, b, :, :].rearrange("p g i -> p (g i)"),
+                in_=live["gn_g", b][:].rearrange("p g i t -> p (g i t)"),
+            )
+
+        def first_matmul(b):
+            m1 = ps.tile([P, CT, P], F32, name="m1", tag="ps")
+            for ct in range(CT):
+                for g in range(G):
+                    nc.tensor.matmul_mx(
+                        out=m1[:, ct, :],
+                        lhsT=hb_q[:, g, ct * P : (ct + 1) * P].bitcast(FP8X4),
+                        lhsT_scale=hb_s[:, g, ct * P : (ct + 1) * P],
+                        rhs=gn_q[:, b, g, :].bitcast(FP8X4),
+                        rhs_scale=gn_s[:, b, g, :],
+                        start=(g == 0),
+                        stop=(g == G - 1),
+                    )
+            live["m1", b] = m1
+
+        def agg_group(b):
+            ag_g = work.tile([P, P, T], BF16, name="ag_g", align_bytes=64)
+            nc.scalar.copy(out=ag_g[:], in_=live["m1", b][:].rearrange("p t i -> p i t"))
+            live["ag_g", b] = ag_g
+
+        def agg_quant(b):
+            ag_q = work.tile([P, P], U32, name="ag_q", align_bytes=64)
+            ag_s = work.tile([P, P], U8, name="ag_s", align_bytes=64)
+            nc.vector.quantize_mx(
+                out=ag_q[:].bitcast(FP8X4), scales=ag_s[:], in_=live["ag_g", b][:].rearrange("p i t -> p (i t)")
+            )
+            live["ag_q", b] = (ag_q, ag_s)
+
+        def second_matmul(b):
+            ag_q, ag_s = live["ag_q", b]
+            m2 = ps.tile([P, D], F32, name="m2", tag="ps")
+            nc.tensor.matmul_mx(
+                out=m2[:],
+                lhsT=ag_q[:].bitcast(FP8X4),
+                lhsT_scale=ag_s[:],
+                rhs=w_q[:].bitcast(FP8X4),
+                rhs_scale=w_s[:],
+                start=True,
+                stop=True,
+            )
+            live["m2", b] = m2
+
+        def finish(b):
+            lin = work.tile([P, D], F32, name="lin")
+            nc.vector.tensor_tensor(out=lin[:], in0=live["m2", b][:], in1=bias_bc[:], op=ALU.add)
+            res = work.tile([P, D], F32, name="res")
+            nc.vector.scalar_tensor_tensor(
+                out=res[:], in0=lin[:], scalar=NEG_SLOPE, in1=lin[:], op0=ALU.mult, op1=ALU.max
+            )
+            nc.sync.dma_start(out=out[b * P : (b + 1) * P, :], in_=res[:])
+
+        setup()
+        vec_columns()
+        for b in range(4):
+            row_sum(b)
+        roots(0)
+        row_sum(4)
+        recip(0)
+        spread(0)
+        for b in range(5, NT):
+            row_sum(b)
+        roots(1)
+        scale(0, 0)
+        scale(1, 0)
+        recip(1)
+        h_turn(0, 0)
+        h_turn(1, 0)
+        spread(1)
+        h_turn(2, 0)
+        h_turn(3, 0)
+        scale(2, 0)
+        scale(3, 0)
+        for b in range(4):
+            scale(b, 1)
+        w_group()
+        for ct in range(CT):
+            h_affine(ct, 0)
+        for ct in range(CT):
+            h_turn(ct, 1)
+        h_affine(0, 1)
+        hb_turn(0)
+        h_affine(1, 1)
+        hb_turn(1)
+        hb_group(0)
+        h_affine(2, 1)
+        hb_turn(2)
+        hb_group(1)
+        h_affine(3, 1)
+        hb_turn(3)
+        hb_group(2)
+        gn_turn(0)
+        gn_turn(1)
+        for b in range(4, NT):
+            scale(b, 0)
+            scale(b, 1)
+        hb_group(3)
+        gn_group(0)
+        hb_quant(0)
+        hb_quant(1)
+        gn_quant(0)
+        first_matmul(0)
+        gn_group(1)
+        w_quant()
+        gn_turn(2)
+        for k in range(NT):
+            agg_group(k)
+            if k + 2 < NT:
+                gn_group(k + 2)
+            if k + 1 < NT:
+                gn_quant(k + 1)
+                first_matmul(k + 1)
+            agg_quant(k)
+            second_matmul(k)
+            if k + 3 < NT:
+                gn_turn(k + 3)
+            if k >= 1:
+                finish(k - 1)
+        finish(NT - 1)

@@ -31,7 +31,7 @@ def tile_tls_msc_pb_kernel(tc, h, adj, gcn_bn_g, gcn_bn_b, gcn_w, gcn_b, out):
     nc = tc.nc
     with ExitStack() as ctx:
         keep = ctx.enter_context(tc.tile_pool(name="keep", bufs=1))
-        work = ctx.enter_context(tc.tile_pool(name="work", bufs=3))
+        work = ctx.enter_context(tc.tile_pool(name="work", bufs=4))
         ps_c = ctx.enter_context(tc.psum_pool(name="ps_c", bufs=1))
         ps = ctx.enter_context(tc.psum_pool(name="ps", bufs=6))
         ctx.enter_context(tc.manual_schedule())
@@ -48,7 +48,6 @@ def tile_tls_msc_pb_kernel(tc, h, adj, gcn_bn_g, gcn_bn_b, gcn_w, gcn_b, out):
         deg_s = keep.tile([P, 4], F32, name="deg_s")
         junk = keep.tile([P, N], BF16, name="junk")
         gd = keep.tile([P, NT, P], F32, name="gd")
-        root = keep.tile([P, NT], F32, name="root")
         dinv = keep.tile([P, NT], F32, name="dinv")
         gb = keep.tile([P, 2 * CT], F32, name="gb")
         hbt = keep.tile([P, CT, NT, P], BF16, name="hbt")
@@ -69,7 +68,7 @@ def tile_tls_msc_pb_kernel(tc, h, adj, gcn_bn_g, gcn_bn_b, gcn_w, gcn_b, out):
             make_identity(nc, ident_f[:])
             nc.vector.memset(vecs[:], 0.0)
             nc.vector.memset(warm[:], 1.0)
-            nc.scalar.activation(out=warm[:], in_=warm[:], func=ACT.Sqrt)
+            nc.scalar.activation(out=warm[:], in_=warm[:], func=ACT.Abs_reciprocal_sqrt)
             nc.scalar.dma_start(out=vecs[0:CT, :], in_=gcn_bn_g.rearrange("(t p) -> t p", p=P))
             nc.scalar.dma_start(out=vecs[CT : 2 * CT, :], in_=gcn_bn_b.rearrange("(t p) -> t p", p=P))
             for b in range(NT):
@@ -99,16 +98,19 @@ def tile_tls_msc_pb_kernel(tc, h, adj, gcn_bn_g, gcn_bn_b, gcn_w, gcn_b, out):
                 out=gd[:, b, :], in0=adj_sb[:, b, b * P : (b + 1) * P], in1=ident_f[:], op=ALU.add
             )
 
-        def roots(q):
+        def inv_roots(q):
             nc.scalar.activation(
-                out=root[:, 4 * q : 4 * q + 2], in_=deg_v[:, 2 * q : 2 * q + 2], func=ACT.Sqrt, bias=1.0
+                out=dinv[:, 4 * q : 4 * q + 2],
+                in_=deg_v[:, 2 * q : 2 * q + 2],
+                func=ACT.Abs_reciprocal_sqrt,
+                bias=1.0,
             )
             nc.scalar.activation(
-                out=root[:, 4 * q + 2 : 4 * q + 4], in_=deg_s[:, 2 * q : 2 * q + 2], func=ACT.Sqrt, bias=1.0
+                out=dinv[:, 4 * q + 2 : 4 * q + 4],
+                in_=deg_s[:, 2 * q : 2 * q + 2],
+                func=ACT.Abs_reciprocal_sqrt,
+                bias=1.0,
             )
-
-        def recip(q):
-            nc.vector.reciprocal(out=dinv[:, 4 * q : 4 * q + 4], in_=root[:, 4 * q : 4 * q + 4])
 
         def spread(q):
             for r in range(4):
@@ -142,13 +144,23 @@ def tile_tls_msc_pb_kernel(tc, h, adj, gcn_bn_g, gcn_bn_b, gcn_w, gcn_b, out):
             live["t1", ct, half] = t1
 
         def h_affine(ct, half):
-            nc.scalar.activation(
-                out=hbt[:, ct, 4 * half : 4 * half + 4, :],
-                in_=live["t1", ct, half][:],
-                func=ACT.Identity,
-                scale=gb[:, ct : ct + 1],
-                bias=gb[:, CT + ct : CT + ct + 1],
-            )
+            if half == 0:
+                nc.scalar.activation(
+                    out=hbt[:, ct, 0:4, :],
+                    in_=live["t1", ct, half][:],
+                    func=ACT.Identity,
+                    scale=gb[:, ct : ct + 1],
+                    bias=gb[:, CT + ct : CT + ct + 1],
+                )
+            else:
+                nc.vector.tensor_scalar(
+                    out=hbt[:, ct, 4:8, :],
+                    in0=live["t1", ct, half][:],
+                    scalar1=gb[:, ct : ct + 1],
+                    scalar2=gb[:, CT + ct : CT + ct + 1],
+                    op0=ALU.mult,
+                    op1=ALU.add,
+                )
 
         def hb_turn(ct):
             t2 = ps.tile([P, NT, P], BF16, name="t2", tag="ps")
@@ -252,66 +264,56 @@ def tile_tls_msc_pb_kernel(tc, h, adj, gcn_bn_g, gcn_bn_b, gcn_w, gcn_b, out):
         vec_columns()
         for b in range(4):
             row_sum(b)
-        roots(0)
-        row_sum(4)
-        recip(0)
+        inv_roots(0)
         spread(0)
-        for b in range(5, NT):
+        for b in range(4, NT):
             row_sum(b)
-        roots(1)
-        scale(0, 0)
-        scale(1, 0)
-        recip(1)
-        h_turn(0, 0)
-        h_turn(1, 0)
+        inv_roots(1)
+        for ct in range(CT):
+            h_turn(ct, 0)
         spread(1)
-        h_turn(2, 0)
-        h_turn(3, 0)
-        scale(2, 0)
-        scale(3, 0)
         for b in range(4):
-            scale(b, 1)
+            scale(b, 0)
         w_group()
         for ct in range(CT):
             h_affine(ct, 0)
         for ct in range(CT):
             h_turn(ct, 1)
-        h_affine(0, 1)
-        hb_turn(0)
-        h_affine(1, 1)
-        hb_turn(1)
-        hb_group(0)
-        h_affine(2, 1)
-        hb_turn(2)
-        hb_group(1)
-        h_affine(3, 1)
-        hb_turn(3)
-        hb_group(2)
-        gn_turn(0)
-        gn_turn(1)
-        for b in range(4, NT):
+        for ct in range(CT):
+            h_affine(ct, 1)
+            hb_turn(ct)
+            scale(ct, 1)
+        for ct in range(CT):
+            hb_group(ct)
+        for b in range(4, 6):
             scale(b, 0)
             scale(b, 1)
-        hb_group(3)
-        gn_group(0)
+        for b in range(4):
+            gn_turn(b)
+        for b in range(3):
+            gn_group(b)
         hb_quant(0)
         hb_quant(1)
         gn_quant(0)
         first_matmul(0)
-        gn_group(1)
         w_quant()
-        gn_turn(2)
-        for k in range(NT):
-            agg_group(k)
-            if k + 2 < NT:
-                gn_group(k + 2)
-            if k + 1 < NT:
-                gn_quant(k + 1)
-                first_matmul(k + 1)
-            agg_quant(k)
-            second_matmul(k)
+        gn_quant(1)
+        first_matmul(1)
+        for k in range(NT + 1):
+            if k + 6 < NT:
+                scale(k + 6, 0)
+                scale(k + 6, 1)
+            if k < NT:
+                agg_group(k)
+            if k + 4 < NT:
+                gn_turn(k + 4)
             if k + 3 < NT:
-                gn_turn(k + 3)
+                gn_group(k + 3)
+            if k + 2 < NT:
+                gn_quant(k + 2)
+                first_matmul(k + 2)
+            if k < NT:
+                agg_quant(k)
+                second_matmul(k)
             if k >= 1:
                 finish(k - 1)
-        finish(NT - 1)

@@ -19,6 +19,7 @@ CT = D // P
 G = 2
 T = 4
 NEG_SLOPE = 0.01
+FOLD = 256
 
 FLOPS = 2 * N * N * D + 2 * N * D * D
 
@@ -46,7 +47,7 @@ def tile_tls_msc_pb_kernel(tc, h, adj, gcn_bn_g, gcn_bn_b, gcn_w, gcn_b, out):
         bias_bc = keep.tile([P, D], BF16, name="bias_bc")
         deg_v = keep.tile([P, 4], F32, name="deg_v")
         deg_s = keep.tile([P, 4], F32, name="deg_s")
-        junk = keep.tile([P, N], BF16, name="junk")
+        junk = keep.tile([P, FOLD], BF16, name="junk")
         gd = keep.tile([P, NT, P], F32, name="gd")
         dinv = keep.tile([P, NT], F32, name="dinv")
         gb = keep.tile([P, 2 * CT], F32, name="gb")
@@ -91,9 +92,16 @@ def tile_tls_msc_pb_kernel(tc, h, adj, gcn_bn_g, gcn_bn_b, gcn_w, gcn_b, out):
                     out=deg_v[:, k : k + 1], in_=adj_sb[:, b, :], axis=mybir.AxisListType.X, op=ALU.add
                 )
             else:
-                nc.scalar.activation(
-                    out=junk[:], in_=adj_sb[:, b, :], func=ACT.Copy, accum_out=deg_s[:, k : k + 1]
-                )
+                fold = ps.tile([P, FOLD], F32, name="fold", tag="ps")
+                for c in range(N // FOLD):
+                    nc.tensor.matmul(
+                        out=fold[:],
+                        lhsT=ident_bf[:],
+                        rhs=adj_sb[:, b, c * FOLD : (c + 1) * FOLD],
+                        start=(c == 0),
+                        stop=(c == N // FOLD - 1),
+                    )
+                nc.scalar.activation(out=junk[:], in_=fold[:], func=ACT.Copy, accum_out=deg_s[:, k : k + 1])
             nc.gpsimd.tensor_tensor(
                 out=gd[:, b, :], in0=adj_sb[:, b, b * P : (b + 1) * P], in1=ident_f[:], op=ALU.add
             )
@@ -265,9 +273,11 @@ def tile_tls_msc_pb_kernel(tc, h, adj, gcn_bn_g, gcn_bn_b, gcn_w, gcn_b, out):
         for b in range(4):
             row_sum(b)
         inv_roots(0)
+        row_sum(4)
+        row_sum(5)
         spread(0)
-        for b in range(4, NT):
-            row_sum(b)
+        row_sum(6)
+        row_sum(7)
         inv_roots(1)
         for ct in range(CT):
             h_turn(ct, 0)

@@ -170,16 +170,17 @@ def tile_tls_msc_pb_kernel(tc, h, adj, gcn_bn_g, gcn_bn_b, gcn_w, gcn_b, out):
                     op1=ALU.add,
                 )
 
-        def hb_turn(ct):
-            t2 = ps.tile([P, NT, P], BF16, name="t2", tag="ps")
-            for a in range(NT):
-                nc.tensor.transpose(out=t2[:, a, :], in_=hbt[:, ct, a, :], identity=ident_bf[:])
-            live["t2", ct] = t2
+        def hb_turn(g, pair):
+            t2 = ps.tile([P, T, 2, P], BF16, name="t2", tag="ps")
+            for t in range(T):
+                for c in range(2):
+                    nc.tensor.transpose(out=t2[:, t, c, :], in_=hbt[:, 2 * pair + c, T * g + t, :], identity=ident_bf[:])
+            live["t2", g, pair] = t2
 
-        def hb_group(ct):
+        def hb_group(g, pair):
             nc.scalar.copy(
-                out=hb_g[:, :, ct * P : (ct + 1) * P, :],
-                in_=live["t2", ct][:].rearrange("p (g t) c -> p g c t", g=G),
+                out=hb_g[:, g, 2 * pair * P : 2 * (pair + 1) * P, :],
+                in_=live["t2", g, pair][:].rearrange("p t l c -> p (l c) t"),
             )
 
         def hb_quant(g):
@@ -259,9 +260,13 @@ def tile_tls_msc_pb_kernel(tc, h, adj, gcn_bn_g, gcn_bn_b, gcn_w, gcn_b, out):
             )
             live["m2", b] = m2
 
-        def finish(b):
+        def add_bias(b):
             lin = work.tile([P, D], F32, name="lin")
             nc.vector.tensor_tensor(out=lin[:], in0=live["m2", b][:], in1=bias_bc[:], op=ALU.add)
+            live["lin", b] = lin
+
+        def leaky(b):
+            lin = live["lin", b]
             res = work.tile([P, D], F32, name="res")
             nc.vector.scalar_tensor_tensor(
                 out=res[:], in0=lin[:], scalar=NEG_SLOPE, in1=lin[:], op0=ALU.mult, op1=ALU.max
@@ -282,34 +287,37 @@ def tile_tls_msc_pb_kernel(tc, h, adj, gcn_bn_g, gcn_bn_b, gcn_w, gcn_b, out):
         for ct in range(CT):
             h_turn(ct, 0)
         spread(1)
-        for b in range(4):
-            scale(b, 0)
         w_group()
-        for ct in range(CT):
-            h_affine(ct, 0)
-        for ct in range(CT):
-            h_turn(ct, 1)
-        for ct in range(CT):
-            h_affine(ct, 1)
-            hb_turn(ct)
-            scale(ct, 1)
-        for ct in range(CT):
-            hb_group(ct)
-        for b in range(4, 6):
-            scale(b, 0)
-            scale(b, 1)
-        for b in range(4):
+        for half in range(2):
+            for pair in range(2):
+                scale(2 * pair, half)
+                scale(2 * pair + 1, half)
+                h_affine(2 * pair, half)
+                h_affine(2 * pair + 1, half)
+                hb_turn(half, pair)
+                if half == 0:
+                    h_turn(2 * pair, 1)
+                    h_turn(2 * pair + 1, 1)
+        for g in range(G):
+            for pair in range(2):
+                hb_group(g, pair)
+        for b in range(3):
             gn_turn(b)
+        scale(4, 0)
+        scale(4, 1)
+        hb_quant(0)
+        scale(5, 0)
+        scale(5, 1)
         for b in range(3):
             gn_group(b)
-        hb_quant(0)
         hb_quant(1)
         gn_quant(0)
         first_matmul(0)
         w_quant()
+        gn_turn(3)
         gn_quant(1)
         first_matmul(1)
-        for k in range(NT + 1):
+        for k in range(NT + 2):
             if k + 6 < NT:
                 scale(k + 6, 0)
                 scale(k + 6, 1)
@@ -321,9 +329,12 @@ def tile_tls_msc_pb_kernel(tc, h, adj, gcn_bn_g, gcn_bn_b, gcn_w, gcn_b, out):
                 gn_group(k + 3)
             if k + 2 < NT:
                 gn_quant(k + 2)
-                first_matmul(k + 2)
             if k < NT:
                 agg_quant(k)
                 second_matmul(k)
-            if k >= 1:
-                finish(k - 1)
+            if k + 2 < NT:
+                first_matmul(k + 2)
+            if 1 <= k <= NT:
+                add_bias(k - 1)
+            if k >= 2:
+                leaky(k - 2)

@@ -170,17 +170,16 @@ def tile_tls_msc_pb_kernel(tc, h, adj, gcn_bn_g, gcn_bn_b, gcn_w, gcn_b, out):
                     op1=ALU.add,
                 )
 
-        def hb_turn(g, pair):
-            t2 = ps.tile([P, T, 2, P], BF16, name="t2", tag="ps")
-            for t in range(T):
-                for c in range(2):
-                    nc.tensor.transpose(out=t2[:, t, c, :], in_=hbt[:, 2 * pair + c, T * g + t, :], identity=ident_bf[:])
-            live["t2", g, pair] = t2
+        def hb_turn(ct):
+            t2 = ps.tile([P, NT, P], BF16, name="t2", tag="ps")
+            for a in range(NT):
+                nc.tensor.transpose(out=t2[:, a, :], in_=hbt[:, ct, a, :], identity=ident_bf[:])
+            live["t2", ct] = t2
 
-        def hb_group(g, pair):
+        def hb_group(ct):
             nc.scalar.copy(
-                out=hb_g[:, g, 2 * pair * P : 2 * (pair + 1) * P, :],
-                in_=live["t2", g, pair][:].rearrange("p t l c -> p (l c) t"),
+                out=hb_g[:, :, ct * P : (ct + 1) * P, :],
+                in_=live["t2", ct][:].rearrange("p (g t) c -> p g c t", g=G),
             )
 
         def hb_quant(g):
@@ -287,34 +286,31 @@ def tile_tls_msc_pb_kernel(tc, h, adj, gcn_bn_g, gcn_bn_b, gcn_w, gcn_b, out):
         for ct in range(CT):
             h_turn(ct, 0)
         spread(1)
+        for b in range(4):
+            scale(b, 0)
         w_group()
-        for half in range(2):
-            for pair in range(2):
-                scale(2 * pair, half)
-                scale(2 * pair + 1, half)
-                h_affine(2 * pair, half)
-                h_affine(2 * pair + 1, half)
-                hb_turn(half, pair)
-                if half == 0:
-                    h_turn(2 * pair, 1)
-                    h_turn(2 * pair + 1, 1)
-        for g in range(G):
-            for pair in range(2):
-                hb_group(g, pair)
-        for b in range(3):
+        for ct in range(CT):
+            h_affine(ct, 0)
+        for ct in range(CT):
+            h_turn(ct, 1)
+        for ct in range(CT):
+            h_affine(ct, 1)
+            hb_turn(ct)
+            scale(ct, 1)
+        for ct in range(CT):
+            hb_group(ct)
+        for b in range(4, 6):
+            scale(b, 0)
+            scale(b, 1)
+        for b in range(4):
             gn_turn(b)
-        scale(4, 0)
-        scale(4, 1)
-        hb_quant(0)
-        scale(5, 0)
-        scale(5, 1)
         for b in range(3):
             gn_group(b)
+        hb_quant(0)
         hb_quant(1)
         gn_quant(0)
         first_matmul(0)
         w_quant()
-        gn_turn(3)
         gn_quant(1)
         first_matmul(1)
         for k in range(NT + 2):
@@ -329,11 +325,10 @@ def tile_tls_msc_pb_kernel(tc, h, adj, gcn_bn_g, gcn_bn_b, gcn_w, gcn_b, out):
                 gn_group(k + 3)
             if k + 2 < NT:
                 gn_quant(k + 2)
+                first_matmul(k + 2)
             if k < NT:
                 agg_quant(k)
                 second_matmul(k)
-            if k + 2 < NT:
-                first_matmul(k + 2)
             if 1 <= k <= NT:
                 add_bias(k - 1)
             if k >= 2:

@@ -17,15 +17,11 @@ D = 512
 NT = N // P
 CT = D // P
 G = 2
+NU = 4
 T = 4
 NEG_SLOPE = 0.01
-FOLD = 256
 
 FLOPS = 2 * N * N * D + 2 * N * D * D
-
-
-def dinv_col(b):
-    return 4 * (b // 4) + 2 * (b % 2) + (b % 4) // 2
 
 
 def tile_tls_msc_pb_kernel(tc, h, adj, gcn_bn_g, gcn_bn_b, gcn_w, gcn_b, out):
@@ -45,10 +41,10 @@ def tile_tls_msc_pb_kernel(tc, h, adj, gcn_bn_g, gcn_bn_b, gcn_w, gcn_b, out):
         h_sb = keep.tile([P, NT, D], BF16, name="h_sb")
         w_sb = keep.tile([P, T, D], BF16, name="w_sb")
         bias_bc = keep.tile([P, D], BF16, name="bias_bc")
-        deg_v = keep.tile([P, 4], F32, name="deg_v")
-        deg_s = keep.tile([P, 4], F32, name="deg_s")
-        junk = keep.tile([P, FOLD], BF16, name="junk")
-        gd = keep.tile([P, NT, P], F32, name="gd")
+        ones = keep.tile([P, 1], BF16, name="ones")
+        deg = keep.tile([P, NT], F32, name="deg")
+        gd = keep.tile([P, NT, 2 * P], F32, name="gd")
+        ident_2 = keep.tile([P, 2, P, 2], F32, name="ident_2")
         dinv = keep.tile([P, NT], F32, name="dinv")
         gb = keep.tile([P, 2 * CT], F32, name="gb")
         hbt = keep.tile([P, CT, NT, P], BF16, name="hbt")
@@ -62,83 +58,88 @@ def tile_tls_msc_pb_kernel(tc, h, adj, gcn_bn_g, gcn_bn_b, gcn_w, gcn_b, out):
         gn_q = keep.tile([P, NT, G, P], U32, name="gn_q", align_bytes=64)
         gn_s = keep.tile([P, NT, G, P], U8, name="gn_s", align_bytes=64)
         dbc = [ps_c.tile([P, 512], F32, name="dbc%d" % i) for i in range(2)]
+        sums = dbc[1][:, 0 : NT * NT]
         live = {}
 
         def setup():
-            make_identity(nc, ident_bf[:])
-            make_identity(nc, ident_f[:])
             nc.vector.memset(vecs[:], 0.0)
-            nc.vector.memset(warm[:], 1.0)
-            nc.scalar.activation(out=warm[:], in_=warm[:], func=ACT.Abs_reciprocal_sqrt)
-            nc.scalar.dma_start(out=vecs[0:CT, :], in_=gcn_bn_g.rearrange("(t p) -> t p", p=P))
-            nc.scalar.dma_start(out=vecs[CT : 2 * CT, :], in_=gcn_bn_b.rearrange("(t p) -> t p", p=P))
-            for b in range(NT):
-                nc.sync.dma_start(out=adj_sb[:, b, :], in_=adj[b * P : (b + 1) * P, :])
+            nc.sync.dma_start(out=vecs[0:CT, :], in_=gcn_bn_g.rearrange("(t p) -> t p", p=P))
+            nc.sync.dma_start(out=vecs[CT : 2 * CT, :], in_=gcn_bn_b.rearrange("(t p) -> t p", p=P))
+            adj_v = adj.rearrange("(u p e) c -> u p e c", u=NU, e=2)
+            for u in range(NU - 1):
+                nc.sync.dma_start(out=adj_sb[:, 2 * u : 2 * u + 2, :], in_=adj_v[u])
+            for e in range(2):
+                nc.sync.dma_start(out=adj_sb[:, NT - 2 + e, :], in_=adj_v[NU - 1, :, e, :])
             h_v = h.rearrange("(a p) c -> p a c", p=P)
             nc.sync.dma_start(out=h_sb[:, 0:4, :], in_=h_v[:, 0:4, :])
             nc.sync.dma_start(out=h_sb[:, 4:8, :], in_=h_v[:, 4:8, :])
             nc.sync.dma_start(out=w_sb[:], in_=gcn_w.rearrange("(t p) d -> p t d", p=P))
             nc.sync.dma_start(out=bias_bc[:], in_=gcn_b.partition_broadcast(P))
+            make_identity(nc, ident_bf[:])
+            make_identity(nc, ident_f[:])
+            nc.vector.memset(warm[:], 1.0)
+            nc.vector.memset(ones[:], 1.0)
+            nc.vector.memset(ident_2[:], 0.0)
+            for e in range(2):
+                nc.vector.tensor_copy(out=ident_2[:, e, :, e], in_=ident_f[:])
+            nc.scalar.activation(out=warm[:], in_=warm[:], func=ACT.Abs_reciprocal_sqrt)
 
         def vec_columns():
             tv = ps.tile([P, NT, P], BF16, name="tv", tag="ps")
             nc.tensor.transpose(out=tv[:, 0, :], in_=vecs[:], identity=ident_bf[:])
-            nc.vector.tensor_copy(out=gb[:], in_=tv[:, 0, 0 : 2 * CT])
+            live["tv"] = tv
 
-        def row_sum(b):
-            k = b // 2
-            if b % 2 == 0:
-                nc.vector.tensor_reduce(
-                    out=deg_v[:, k : k + 1], in_=adj_sb[:, b, :], axis=mybir.AxisListType.X, op=ALU.add
+        def vec_copy():
+            nc.vector.tensor_copy(out=gb[:], in_=live["tv"][:, 0, 0 : 2 * CT])
+
+        def column_sums(a):
+            u, e = divmod(a, 2)
+            for b in range(NT):
+                first = 2 * P * (b // 2) + b % 2
+                nc.tensor.matmul(
+                    out=sums[:, a * NT + b : a * NT + b + 1],
+                    lhsT=adj_sb[:, a, first : 2 * P * (b // 2 + 1) : 2],
+                    rhs=ones[:],
+                    start=True,
+                    stop=True,
                 )
-            else:
-                fold = ps.tile([P, FOLD], F32, name="fold", tag="ps")
-                for c in range(N // FOLD):
-                    nc.tensor.matmul(
-                        out=fold[:],
-                        lhsT=ident_bf[:],
-                        rhs=adj_sb[:, b, c * FOLD : (c + 1) * FOLD],
-                        start=(c == 0),
-                        stop=(c == N // FOLD - 1),
-                    )
-                nc.scalar.activation(out=junk[:], in_=fold[:], func=ACT.Copy, accum_out=deg_s[:, k : k + 1])
             nc.gpsimd.tensor_tensor(
-                out=gd[:, b, :], in0=adj_sb[:, b, b * P : (b + 1) * P], in1=ident_f[:], op=ALU.add
+                out=gd[:, a, :],
+                in0=adj_sb[:, a, 2 * P * u : 2 * P * (u + 1)],
+                in1=ident_2[:, e, :, :].rearrange("p n e -> p (n e)"),
+                op=ALU.add,
             )
 
-        def inv_roots(q):
-            nc.scalar.activation(
-                out=dinv[:, 4 * q : 4 * q + 2],
-                in_=deg_v[:, 2 * q : 2 * q + 2],
-                func=ACT.Abs_reciprocal_sqrt,
-                bias=1.0,
+        def inv_roots():
+            nc.vector.tensor_reduce(
+                out=deg[:],
+                in_=sums[:].rearrange("p (a b) -> p b a", b=NT),
+                axis=mybir.AxisListType.X,
+                op=ALU.add,
             )
-            nc.scalar.activation(
-                out=dinv[:, 4 * q + 2 : 4 * q + 4],
-                in_=deg_s[:, 2 * q : 2 * q + 2],
-                func=ACT.Abs_reciprocal_sqrt,
-                bias=1.0,
-            )
+            nc.scalar.activation(out=dinv[:], in_=deg[:], func=ACT.Abs_reciprocal_sqrt, bias=1.0)
 
         def spread(q):
             for r in range(4):
-                c = dinv_col(4 * q + r)
+                c = 4 * q + r
+                first = 2 * P * (r // 2) + r % 2
                 nc.tensor.transpose(
-                    out=dbc[q][:, r * P : (r + 1) * P],
+                    out=dbc[q][:, first : 2 * P * (r // 2 + 1) : 2],
                     in_=dinv[:, c : c + 1].to_broadcast([P, P]),
                     identity=ident_f[:],
                 )
 
-        def scale(b, half):
-            c = dinv_col(b)
-            cuts = sorted(set([512 * half, 512 * half + 512] + [x for x in (b * P, (b + 1) * P) if x // 512 == half]))
+        def scale(r):
+            start = 2 * P * (r // 2)
+            cuts = sorted(set([start, start + 2 * P, max(start + 2 * P, 512), N]))
             for lo, hi in zip(cuts[:-1], cuts[1:]):
-                src = gd[:, b, :] if lo == b * P else adj_sb[:, b, lo:hi]
+                src = gd[:, r, :] if lo == start else adj_sb[:, r, lo:hi]
+                bank = dbc[lo // 512][:, lo % 512 : lo % 512 + hi - lo]
                 nc.vector.scalar_tensor_tensor(
-                    out=gn[:, b, lo:hi],
+                    out=gn[:, r, lo:hi],
                     in0=src,
-                    scalar=dinv[:, c : c + 1],
-                    in1=dbc[half][:, lo - 512 * half : hi - 512 * half],
+                    scalar=dinv[:, r : r + 1],
+                    in1=bank,
                     op0=ALU.mult,
                     op1=ALU.mult,
                 )
@@ -152,9 +153,10 @@ def tile_tls_msc_pb_kernel(tc, h, adj, gcn_bn_g, gcn_bn_b, gcn_w, gcn_b, out):
             live["t1", ct, half] = t1
 
         def h_affine(ct, half):
+            a = 4 * half
             if half == 0:
                 nc.scalar.activation(
-                    out=hbt[:, ct, 0:4, :],
+                    out=hbt[:, ct, a : a + 4, :],
                     in_=live["t1", ct, half][:],
                     func=ACT.Identity,
                     scale=gb[:, ct : ct + 1],
@@ -162,7 +164,7 @@ def tile_tls_msc_pb_kernel(tc, h, adj, gcn_bn_g, gcn_bn_b, gcn_w, gcn_b, out):
                 )
             else:
                 nc.vector.tensor_scalar(
-                    out=hbt[:, ct, 4:8, :],
+                    out=hbt[:, ct, a : a + 4, :],
                     in0=live["t1", ct, half][:],
                     scalar1=gb[:, ct : ct + 1],
                     scalar2=gb[:, CT + ct : CT + ct + 1],
@@ -171,15 +173,17 @@ def tile_tls_msc_pb_kernel(tc, h, adj, gcn_bn_g, gcn_bn_b, gcn_w, gcn_b, out):
                 )
 
         def hb_turn(ct):
-            t2 = ps.tile([P, NT, P], BF16, name="t2", tag="ps")
-            for a in range(NT):
-                nc.tensor.transpose(out=t2[:, a, :], in_=hbt[:, ct, a, :], identity=ident_bf[:])
+            t2 = ps.tile([P, NU, P], F32, name="t2", tag="ps")
+            words = hbt[:, ct, :, :].rearrange("p a j -> p (a j)").bitcast(F32)
+            for u in range(NU):
+                nc.tensor.transpose(out=t2[:, u, :], in_=words[:, u * P : (u + 1) * P], identity=ident_f[:])
             live["t2", ct] = t2
 
         def hb_group(ct):
+            words = hb_g[:].rearrange("p g c t -> p (g c t)").bitcast(F32).rearrange("p (g c u) -> p g c u", g=G, u=2)
             nc.scalar.copy(
-                out=hb_g[:, :, ct * P : (ct + 1) * P, :],
-                in_=live["t2", ct][:].rearrange("p (g t) c -> p g c t", g=G),
+                out=words[:, :, ct * P : (ct + 1) * P, :],
+                in_=live["t2", ct][:].rearrange("p (g u) c -> p g c u", g=G),
             )
 
         def hb_quant(g):
@@ -199,16 +203,32 @@ def tile_tls_msc_pb_kernel(tc, h, adj, gcn_bn_g, gcn_bn_b, gcn_w, gcn_b, out):
                 out=w_q[:].bitcast(FP8X4), scales=w_s[:], in_=w_g[:].rearrange("p d t -> p (d t)")
             )
 
-        def gn_turn(b):
-            t3 = ps.tile([P, NT, P], BF16, name="t3", tag="ps")
-            for a in range(NT):
-                nc.tensor.transpose(out=t3[:, a, :], in_=gn[:, b, a * P : (a + 1) * P], identity=ident_bf[:])
-            live["t3", b] = t3
+        def gn_turn(r):
+            group, e = divmod(r, 2)
+            t3 = ps.tile([P, NU, P], F32, name="t3", tag="ps")
+            pairs = t3[:].rearrange("p u i -> p (u i)").bitcast(BF16)
+            rows = gn[:].rearrange("p (u f) c -> p u f c", f=2)
+            for u in range(0, group, 2):
+                n = min(2, group - u)
+                nc.tensor.matmul(
+                    out=pairs[:, 2 * P * u : 2 * P * (u + n)],
+                    lhsT=ident_bf[:],
+                    rhs=rows[:, u : u + n, :, 2 * P * group + e : 2 * P * (group + 1) : 2].rearrange(
+                        "p u f i -> p u i f"
+                    ),
+                    start=True,
+                    stop=True,
+                )
+            words = gn[:, r, :].bitcast(F32)
+            for u in range(group, NU):
+                nc.tensor.transpose(out=t3[:, u, :], in_=words[:, u * P : (u + 1) * P], identity=ident_f[:])
+            live["t3", r] = t3
 
-        def gn_group(b):
+        def gn_group(r):
             gn_g = work.tile([P, G, P, T], BF16, name="gn_g", align_bytes=64)
-            nc.scalar.copy(out=gn_g[:], in_=live["t3", b][:].rearrange("p (g t) i -> p g i t", g=G))
-            live["gn_g", b] = gn_g
+            words = gn_g[:].rearrange("p g i t -> p (g i t)").bitcast(F32).rearrange("p (g i u) -> p g i u", g=G, u=2)
+            nc.scalar.copy(out=words, in_=live["t3", r][:].rearrange("p (g u) i -> p g i u", g=G))
+            live["gn_g", r] = gn_g
 
         def gn_quant(b):
             nc.vector.quantize_mx(
@@ -270,62 +290,54 @@ def tile_tls_msc_pb_kernel(tc, h, adj, gcn_bn_g, gcn_bn_b, gcn_w, gcn_b, out):
             nc.vector.scalar_tensor_tensor(
                 out=res[:], in0=lin[:], scalar=NEG_SLOPE, in1=lin[:], op0=ALU.mult, op1=ALU.max
             )
-            nc.sync.dma_start(out=out[b * P : (b + 1) * P, :], in_=res[:])
+            out_v = out.rearrange("(u p e) d -> u e p d", u=NU, e=2)
+            nc.sync.dma_start(out=out_v[b // 2, b % 2], in_=res[:])
 
         setup()
         vec_columns()
-        for b in range(4):
-            row_sum(b)
-        inv_roots(0)
-        row_sum(4)
-        row_sum(5)
+        vec_copy()
+        for a in range(NT):
+            column_sums(a)
+        inv_roots()
         spread(0)
-        row_sum(6)
-        row_sum(7)
-        inv_roots(1)
-        for ct in range(CT):
-            h_turn(ct, 0)
         spread(1)
-        for b in range(4):
-            scale(b, 0)
+        for half in range(2):
+            for ct in range(CT):
+                h_turn(ct, half)
         w_group()
+        scale(0)
+        scale(1)
+        for half in range(2):
+            for ct in range(CT):
+                h_affine(ct, half)
+        gn_turn(0)
+        gn_group(0)
         for ct in range(CT):
-            h_affine(ct, 0)
-        for ct in range(CT):
-            h_turn(ct, 1)
-        for ct in range(CT):
-            h_affine(ct, 1)
             hb_turn(ct)
-            scale(ct, 1)
+        gn_turn(1)
+        scale(2)
+        scale(3)
         for ct in range(CT):
             hb_group(ct)
-        for b in range(4, 6):
-            scale(b, 0)
-            scale(b, 1)
-        for b in range(4):
-            gn_turn(b)
-        for b in range(3):
-            gn_group(b)
+        gn_turn(2)
+        gn_group(1)
+        gn_group(2)
         hb_quant(0)
         hb_quant(1)
         gn_quant(0)
         first_matmul(0)
         w_quant()
-        gn_quant(1)
-        first_matmul(1)
         for k in range(NT + 2):
-            if k + 6 < NT:
-                scale(k + 6, 0)
-                scale(k + 6, 1)
+            if k + 4 < NT:
+                scale(k + 4)
             if k < NT:
                 agg_group(k)
-            if k + 4 < NT:
-                gn_turn(k + 4)
             if k + 3 < NT:
+                gn_turn(k + 3)
                 gn_group(k + 3)
-            if k + 2 < NT:
-                gn_quant(k + 2)
-                first_matmul(k + 2)
+            if k + 1 < NT:
+                gn_quant(k + 1)
+                first_matmul(k + 1)
             if k < NT:
                 agg_quant(k)
                 second_matmul(k)

@@ -35,19 +35,21 @@ def tile_tls_msc_pb_kernel(tc, h, adj, gcn_bn_g, gcn_bn_b, gcn_w, gcn_b, out):
 
         ident_bf = keep.tile([P, P], BF16, name="ident_bf")
         ident_f = keep.tile([P, P], F32, name="ident_f")
-        vecs = keep.tile([P, P], BF16, name="vecs")
+        vecs = keep.tile([P, 2 * P], BF16, name="vecs")
         warm = keep.tile([P, 1], F32, name="warm")
         adj_sb = keep.tile([P, NT, N], BF16, name="adj_sb")
         h_sb = keep.tile([P, NT, D], BF16, name="h_sb")
         w_sb = keep.tile([P, T, D], BF16, name="w_sb")
         bias_bc = keep.tile([P, D], BF16, name="bias_bc")
         ones = keep.tile([P, 1], BF16, name="ones")
+        row_part = keep.tile([P, NT], F32, name="row_part")
+        junk = keep.tile([P, N], BF16, name="junk")
         deg = keep.tile([P, NT], F32, name="deg")
         gd = keep.tile([P, NT, 2 * P], F32, name="gd")
         ident_2 = keep.tile([P, 2, P, 2], F32, name="ident_2")
         dinv = keep.tile([P, NT], F32, name="dinv")
         gb = keep.tile([P, 2 * CT], F32, name="gb")
-        hbt = keep.tile([P, CT, NT, P], BF16, name="hbt")
+        hbt = keep.tile([P, 2, 2, N], BF16, name="hbt")
         hb_g = keep.tile([P, G, D, T], BF16, name="hb_g", align_bytes=64)
         hb_q = keep.tile([P, G, D], U32, name="hb_q", align_bytes=64)
         hb_s = keep.tile([P, G, D], U8, name="hb_s", align_bytes=64)
@@ -58,22 +60,20 @@ def tile_tls_msc_pb_kernel(tc, h, adj, gcn_bn_g, gcn_bn_b, gcn_w, gcn_b, out):
         gn_q = keep.tile([P, NT, G, P], U32, name="gn_q", align_bytes=64)
         gn_s = keep.tile([P, NT, G, P], U8, name="gn_s", align_bytes=64)
         dbc = [ps_c.tile([P, 512], F32, name="dbc%d" % i) for i in range(2)]
-        sums = dbc[1][:, 0 : NT * NT]
         live = {}
 
         def setup():
             nc.vector.memset(vecs[:], 0.0)
-            nc.sync.dma_start(out=vecs[0:CT, :], in_=gcn_bn_g.rearrange("(t p) -> t p", p=P))
-            nc.sync.dma_start(out=vecs[CT : 2 * CT, :], in_=gcn_bn_b.rearrange("(t p) -> t p", p=P))
+            nc.sync.dma_start(out=vecs[0:2, :], in_=gcn_bn_g.rearrange("(w c) -> w c", w=2))
+            nc.sync.dma_start(out=vecs[2:4, :], in_=gcn_bn_b.rearrange("(w c) -> w c", w=2))
             adj_v = adj.rearrange("(u p e) c -> u p e c", u=NU, e=2)
-            for u in range(NU - 1):
-                nc.sync.dma_start(out=adj_sb[:, 2 * u : 2 * u + 2, :], in_=adj_v[u])
-            for e in range(2):
-                nc.sync.dma_start(out=adj_sb[:, NT - 2 + e, :], in_=adj_v[NU - 1, :, e, :])
+            for u in range(NU):
+                c = 2 * P * u
+                nc.sync.dma_start(out=adj_sb[:, 2 * u : 2 * u + 2, c:N], in_=adj_v[u, :, :, c:N])
             h_v = h.rearrange("(a p) c -> p a c", p=P)
             nc.sync.dma_start(out=h_sb[:, 0:4, :], in_=h_v[:, 0:4, :])
             nc.sync.dma_start(out=h_sb[:, 4:8, :], in_=h_v[:, 4:8, :])
-            nc.sync.dma_start(out=w_sb[:], in_=gcn_w.rearrange("(t p) d -> p t d", p=P))
+            nc.sync.dma_start(out=w_sb[:].rearrange("p (w e) d -> p w (e d)", e=2), in_=gcn_w.rearrange("(w p e) d -> p w (e d)", p=P, e=2))
             nc.sync.dma_start(out=bias_bc[:], in_=gcn_b.partition_broadcast(P))
             make_identity(nc, ident_bf[:])
             make_identity(nc, ident_f[:])
@@ -85,39 +85,48 @@ def tile_tls_msc_pb_kernel(tc, h, adj, gcn_bn_g, gcn_bn_b, gcn_w, gcn_b, out):
             nc.scalar.activation(out=warm[:], in_=warm[:], func=ACT.Abs_reciprocal_sqrt)
 
         def vec_columns():
-            tv = ps.tile([P, NT, P], BF16, name="tv", tag="ps")
-            nc.tensor.transpose(out=tv[:, 0, :], in_=vecs[:], identity=ident_bf[:])
-            live["tv"] = tv
+            tv = ps.tile([P, P], F32, name="tv", tag="ps")
+            nc.tensor.transpose(out=tv[:], in_=vecs[:].bitcast(F32), identity=ident_f[:])
+            nc.vector.tensor_copy(out=gb[:], in_=tv[:].bitcast(BF16)[:, 0:8])
 
-        def vec_copy():
-            nc.vector.tensor_copy(out=gb[:], in_=live["tv"][:, 0, 0 : 2 * CT])
+        def row_sum(r):
+            right = adj_sb[:, r, 2 * P * (r // 2 + 1) : N]
+            part = row_part[:, r : r + 1]
+            if r % 2 == 0:
+                nc.vector.tensor_reduce(out=part, in_=right, axis=mybir.AxisListType.X, op=ALU.add)
+            else:
+                width = right.shape[1]
+                nc.scalar.activation(out=junk[:, 0:width], in_=right, func=ACT.Copy, accum_out=part)
 
-        def column_sums(a):
-            u, e = divmod(a, 2)
-            for b in range(NT):
-                first = 2 * P * (b // 2) + b % 2
-                nc.tensor.matmul(
-                    out=sums[:, a * NT + b : a * NT + b + 1],
-                    lhsT=adj_sb[:, a, first : 2 * P * (b // 2 + 1) : 2],
-                    rhs=ones[:],
-                    start=True,
-                    stop=True,
+        def column_sums(u):
+            for e in range(2):
+                r = 2 * u + e
+                for a in range(2 * u + 2):
+                    nc.tensor.matmul(
+                        out=live["sums"][:, r : r + 1],
+                        lhsT=adj_sb[:, a, 2 * P * u + e : 2 * P * (u + 1) : 2],
+                        rhs=ones[:],
+                        start=(a == 0),
+                        stop=(a == 2 * u + 1),
+                    )
+                nc.gpsimd.tensor_tensor(
+                    out=gd[:, r, :],
+                    in0=adj_sb[:, r, 2 * P * u : 2 * P * (u + 1)],
+                    in1=ident_2[:, e, :, :].rearrange("p n e -> p (n e)"),
+                    op=ALU.add,
                 )
-            nc.gpsimd.tensor_tensor(
-                out=gd[:, a, :],
-                in0=adj_sb[:, a, 2 * P * u : 2 * P * (u + 1)],
-                in1=ident_2[:, e, :, :].rearrange("p n e -> p (n e)"),
-                op=ALU.add,
-            )
 
-        def inv_roots():
-            nc.vector.tensor_reduce(
-                out=deg[:],
-                in_=sums[:].rearrange("p (a b) -> p b a", b=NT),
-                axis=mybir.AxisListType.X,
-                op=ALU.add,
+        def inv_roots(q):
+            c = 4 * q
+            n = 4 if q == 0 else 2
+            nc.vector.tensor_tensor(
+                out=deg[:, c : c + n], in0=live["sums"][:, c : c + n], in1=row_part[:, c : c + n], op=ALU.add
             )
-            nc.scalar.activation(out=dinv[:], in_=deg[:], func=ACT.Abs_reciprocal_sqrt, bias=1.0)
+            if q == 1:
+                nc.vector.tensor_copy(out=deg[:, 6:8], in_=live["sums"][:, 6:8])
+            nc.scalar.activation(
+                out=dinv[:, c : c + 4], in_=deg[:, c : c + 4], func=ACT.Abs_reciprocal_sqrt, bias=1.0
+            )
 
         def spread(q):
             for r in range(4):
@@ -144,37 +153,42 @@ def tile_tls_msc_pb_kernel(tc, h, adj, gcn_bn_g, gcn_bn_b, gcn_w, gcn_b, out):
                     op1=ALU.mult,
                 )
 
-        def h_turn(ct, half):
-            t1 = ps.tile([P, 4, P], BF16, name="t1", tag="ps")
+        def h_turn(w, half):
+            t1 = ps.tile([P, 4, P], F32, name="t1", tag="ps")
             for a in range(4):
                 nc.tensor.transpose(
-                    out=t1[:, a, :], in_=h_sb[:, 4 * half + a, ct * P : (ct + 1) * P], identity=ident_bf[:]
+                    out=t1[:, a, :],
+                    in_=h_sb[:, 4 * half + a, :].bitcast(F32)[:, w * P : (w + 1) * P],
+                    identity=ident_f[:],
                 )
-            live["t1", ct, half] = t1
+            live["t1", w, half] = t1
 
-        def h_affine(ct, half):
-            a = 4 * half
-            if half == 0:
-                nc.scalar.activation(
-                    out=hbt[:, ct, a : a + 4, :],
-                    in_=live["t1", ct, half][:],
-                    func=ACT.Identity,
-                    scale=gb[:, ct : ct + 1],
-                    bias=gb[:, CT + ct : CT + ct + 1],
-                )
-            else:
+        def h_affine(w, half, e):
+            src = live["t1", w, half][:].rearrange("p a n -> p (a n)").bitcast(BF16)
+            src = src.rearrange("p (n e) -> p e n", e=2)[:, e, :]
+            dst = hbt[:, w, e, 512 * half : 512 * (half + 1)]
+            c = 2 * w + e
+            if (w, half) == (1, 1):
                 nc.vector.tensor_scalar(
-                    out=hbt[:, ct, a : a + 4, :],
-                    in0=live["t1", ct, half][:],
-                    scalar1=gb[:, ct : ct + 1],
-                    scalar2=gb[:, CT + ct : CT + ct + 1],
+                    out=dst,
+                    in0=src,
+                    scalar1=gb[:, c : c + 1],
+                    scalar2=gb[:, CT + c : CT + c + 1],
                     op0=ALU.mult,
                     op1=ALU.add,
+                )
+            else:
+                nc.scalar.activation(
+                    out=dst,
+                    in_=src,
+                    func=ACT.Identity,
+                    scale=gb[:, c : c + 1],
+                    bias=gb[:, CT + c : CT + c + 1],
                 )
 
         def hb_turn(ct):
             t2 = ps.tile([P, NU, P], F32, name="t2", tag="ps")
-            words = hbt[:, ct, :, :].rearrange("p a j -> p (a j)").bitcast(F32)
+            words = hbt[:, ct // 2, ct % 2, :].bitcast(F32)
             for u in range(NU):
                 nc.tensor.transpose(out=t2[:, u, :], in_=words[:, u * P : (u + 1) * P], identity=ident_f[:])
             live["t2", ct] = t2
@@ -295,46 +309,52 @@ def tile_tls_msc_pb_kernel(tc, h, adj, gcn_bn_g, gcn_bn_b, gcn_w, gcn_b, out):
 
         setup()
         vec_columns()
-        vec_copy()
-        for a in range(NT):
-            column_sums(a)
-        inv_roots()
+        live["sums"] = ps.tile([P, NT], F32, name="sums", tag="ps")
+        for u in range(3):
+            row_sum(2 * u)
+            row_sum(2 * u + 1)
+            column_sums(u)
+            if u == 1:
+                inv_roots(0)
+        column_sums(3)
+        inv_roots(1)
         spread(0)
         spread(1)
-        for half in range(2):
-            for ct in range(CT):
-                h_turn(ct, half)
         w_group()
+        for w in range(2):
+            h_turn(w, 0)
+        for w in range(2):
+            h_turn(w, 1)
         scale(0)
         scale(1)
-        for half in range(2):
-            for ct in range(CT):
-                h_affine(ct, half)
         gn_turn(0)
-        gn_group(0)
+        for half in range(2):
+            for w in range(2):
+                for e in range(2):
+                    h_affine(w, half, e)
         for ct in range(CT):
             hb_turn(ct)
-        gn_turn(1)
-        scale(2)
-        scale(3)
-        for ct in range(CT):
             hb_group(ct)
+        gn_turn(1)
+        for r in range(2, 6):
+            scale(r)
         gn_turn(2)
+        gn_group(0)
         gn_group(1)
-        gn_group(2)
         hb_quant(0)
         hb_quant(1)
         gn_quant(0)
         first_matmul(0)
         w_quant()
         for k in range(NT + 2):
-            if k + 4 < NT:
-                scale(k + 4)
+            if k + 6 < NT:
+                scale(k + 6)
             if k < NT:
                 agg_group(k)
             if k + 3 < NT:
                 gn_turn(k + 3)
-                gn_group(k + 3)
+            if k + 2 < NT:
+                gn_group(k + 2)
             if k + 1 < NT:
                 gn_quant(k + 1)
                 first_matmul(k + 1)

@@ -321,46 +321,55 @@ def tile_tls_msc_pb_kernel(tc, h, adj, gcn_bn_g, gcn_bn_b, gcn_w, gcn_b, out):
         spread(0)
         spread(1)
         w_group()
-        for w in range(2):
-            h_turn(w, 0)
-        for w in range(2):
-            h_turn(w, 1)
-        scale(0)
-        scale(1)
-        gn_turn(0)
         for half in range(2):
             for w in range(2):
-                for e in range(2):
-                    h_affine(w, half, e)
+                h_turn(w, half)
+        scale(0)
+        scale(1)
+        for w in range(2):
+            for e in range(2):
+                h_affine(w, 0, e)
+        gn_turn(0)
+        gn_group(0)
+        scale(2)
+        scale(3)
+        gn_turn(1)
+        gn_group(1)
+        for w in range(2):
+            for e in range(2):
+                h_affine(w, 1, e)
+        for r in range(4, NT):
+            scale(r)
         for ct in range(CT):
             hb_turn(ct)
             hb_group(ct)
-        gn_turn(1)
+        gn_quant(0)
+        gn_quant(1)
         for r in range(2, 6):
-            scale(r)
-        gn_turn(2)
-        gn_group(0)
-        gn_group(1)
+            gn_turn(r)
+            if r < 4:
+                gn_group(r)
         hb_quant(0)
         hb_quant(1)
-        gn_quant(0)
+        gn_quant(2)
         first_matmul(0)
+        gn_quant(3)
         w_quant()
+        first_matmul(1)
         for k in range(NT + 2):
-            if k + 6 < NT:
-                scale(k + 6)
             if k < NT:
                 agg_group(k)
-            if k + 3 < NT:
-                gn_turn(k + 3)
-            if k + 2 < NT:
-                gn_group(k + 2)
-            if k + 1 < NT:
-                gn_quant(k + 1)
-                first_matmul(k + 1)
+            if k + 4 < NT:
+                gn_group(k + 4)
             if k < NT:
                 agg_quant(k)
                 second_matmul(k)
+            if k + 4 < NT:
+                gn_quant(k + 4)
+            if k + 2 < NT:
+                first_matmul(k + 2)
+            if k + 6 < NT:
+                gn_turn(k + 6)
             if 1 <= k <= NT:
                 add_bias(k - 1)
             if k >= 2:

@@ -29,6 +29,7 @@ def tile_tls_msc_pb_kernel(tc, h, adj, gcn_bn_g, gcn_bn_b, gcn_w, gcn_b, out):
     with ExitStack() as ctx:
         keep = ctx.enter_context(tc.tile_pool(name="keep", bufs=1))
         work = ctx.enter_context(tc.tile_pool(name="work", bufs=4))
+        eight = ctx.enter_context(tc.tile_pool(name="eight", bufs=NT))
         ps_c = ctx.enter_context(tc.psum_pool(name="ps_c", bufs=1))
         ps = ctx.enter_context(tc.psum_pool(name="ps", bufs=6))
         ctx.enter_context(tc.manual_schedule())
@@ -42,8 +43,8 @@ def tile_tls_msc_pb_kernel(tc, h, adj, gcn_bn_g, gcn_bn_b, gcn_w, gcn_b, out):
         w_sb = keep.tile([P, T, D], BF16, name="w_sb")
         bias_bc = keep.tile([P, D], BF16, name="bias_bc")
         ones = keep.tile([P, 1], BF16, name="ones")
-        row_part = keep.tile([P, NT], F32, name="row_part")
-        junk = keep.tile([P, N], BF16, name="junk")
+        row_part = keep.tile([P, 4], F32, name="row_part")
+        junk = keep.tile([P, 512], BF16, name="junk")
         deg = keep.tile([P, NT], F32, name="deg")
         gd = keep.tile([P, NT, 2 * P], F32, name="gd")
         ident_2 = keep.tile([P, 2, P, 2], F32, name="ident_2")
@@ -68,7 +69,7 @@ def tile_tls_msc_pb_kernel(tc, h, adj, gcn_bn_g, gcn_bn_b, gcn_w, gcn_b, out):
             nc.sync.dma_start(out=vecs[2:4, :], in_=gcn_bn_b.rearrange("(w c) -> w c", w=2))
             adj_v = adj.rearrange("(u p e) c -> u p e c", u=NU, e=2)
             for u in range(NU):
-                c = 2 * P * u
+                c = 512 * (u // 2)
                 nc.sync.dma_start(out=adj_sb[:, 2 * u : 2 * u + 2, c:N], in_=adj_v[u, :, :, c:N])
             h_v = h.rearrange("(a p) c -> p a c", p=P)
             nc.sync.dma_start(out=h_sb[:, 0:4, :], in_=h_v[:, 0:4, :])
@@ -90,43 +91,41 @@ def tile_tls_msc_pb_kernel(tc, h, adj, gcn_bn_g, gcn_bn_b, gcn_w, gcn_b, out):
             nc.vector.tensor_copy(out=gb[:], in_=tv[:].bitcast(BF16)[:, 0:8])
 
         def row_sum(r):
-            right = adj_sb[:, r, 2 * P * (r // 2 + 1) : N]
+            right = adj_sb[:, r, 512:N]
             part = row_part[:, r : r + 1]
             if r % 2 == 0:
                 nc.vector.tensor_reduce(out=part, in_=right, axis=mybir.AxisListType.X, op=ALU.add)
             else:
-                width = right.shape[1]
-                nc.scalar.activation(out=junk[:, 0:width], in_=right, func=ACT.Copy, accum_out=part)
+                nc.scalar.activation(out=junk[:], in_=right, func=ACT.Copy, accum_out=part)
 
-        def column_sums(u):
-            for e in range(2):
-                r = 2 * u + e
-                for a in range(2 * u + 2):
-                    nc.tensor.matmul(
-                        out=live["sums"][:, r : r + 1],
-                        lhsT=adj_sb[:, a, 2 * P * u + e : 2 * P * (u + 1) : 2],
-                        rhs=ones[:],
-                        start=(a == 0),
-                        stop=(a == 2 * u + 1),
-                    )
-                nc.gpsimd.tensor_tensor(
-                    out=gd[:, r, :],
-                    in0=adj_sb[:, r, 2 * P * u : 2 * P * (u + 1)],
-                    in1=ident_2[:, e, :, :].rearrange("p n e -> p (n e)"),
-                    op=ALU.add,
+        def with_identity(r):
+            u, e = divmod(r, 2)
+            nc.gpsimd.tensor_tensor(
+                out=gd[:, r, :],
+                in0=adj_sb[:, r, 2 * P * u : 2 * P * (u + 1)],
+                in1=ident_2[:, e, :, :].rearrange("p n e -> p (n e)"),
+                op=ALU.add,
+            )
+
+        def column_sums(r):
+            u, e = divmod(r, 2)
+            last = 4 * (r // 4) + 3
+            for a in range(last + 1):
+                nc.tensor.matmul(
+                    out=live["sums"][:, r : r + 1],
+                    lhsT=adj_sb[:, a, 2 * P * u + e : 2 * P * (u + 1) : 2],
+                    rhs=ones[:],
+                    start=(a == 0),
+                    stop=(a == last),
                 )
 
         def inv_roots(q):
-            c = 4 * q
-            n = 4 if q == 0 else 2
-            nc.vector.tensor_tensor(
-                out=deg[:, c : c + n], in0=live["sums"][:, c : c + n], in1=row_part[:, c : c + n], op=ALU.add
-            )
-            if q == 1:
-                nc.vector.tensor_copy(out=deg[:, 6:8], in_=live["sums"][:, 6:8])
-            nc.scalar.activation(
-                out=dinv[:, c : c + 4], in_=deg[:, c : c + 4], func=ACT.Abs_reciprocal_sqrt, bias=1.0
-            )
+            c = slice(4 * q, 4 * q + 4)
+            if q == 0:
+                nc.vector.tensor_tensor(out=deg[:, c], in0=live["sums"][:, c], in1=row_part[:], op=ALU.add)
+            else:
+                nc.vector.tensor_copy(out=deg[:, c], in_=live["sums"][:, c])
+            nc.scalar.activation(out=dinv[:, c], in_=deg[:, c], func=ACT.Abs_reciprocal_sqrt, bias=1.0)
 
         def spread(q):
             for r in range(4):
@@ -139,10 +138,11 @@ def tile_tls_msc_pb_kernel(tc, h, adj, gcn_bn_g, gcn_bn_b, gcn_w, gcn_b, out):
                 )
 
         def scale(r):
-            start = 2 * P * (r // 2)
-            cuts = sorted(set([start, start + 2 * P, max(start + 2 * P, 512), N]))
+            half = 512 * (r // 4)
+            diag = 2 * P * (r // 2)
+            cuts = sorted(set([half, diag, diag + 2 * P, half + 512, N]))
             for lo, hi in zip(cuts[:-1], cuts[1:]):
-                src = gd[:, r, :] if lo == start else adj_sb[:, r, lo:hi]
+                src = gd[:, r, :] if lo == diag else adj_sb[:, r, lo:hi]
                 bank = dbc[lo // 512][:, lo % 512 : lo % 512 + hi - lo]
                 nc.vector.scalar_tensor_tensor(
                     out=gn[:, r, lo:hi],
@@ -218,31 +218,35 @@ def tile_tls_msc_pb_kernel(tc, h, adj, gcn_bn_g, gcn_bn_b, gcn_w, gcn_b, out):
             )
 
         def gn_turn(r):
-            group, e = divmod(r, 2)
+            first = 2 * (r // 4)
             t3 = ps.tile([P, NU, P], F32, name="t3", tag="ps")
-            pairs = t3[:].rearrange("p u i -> p (u i)").bitcast(BF16)
-            rows = gn[:].rearrange("p (u f) c -> p u f c", f=2)
-            for u in range(0, group, 2):
-                n = min(2, group - u)
-                nc.tensor.matmul(
-                    out=pairs[:, 2 * P * u : 2 * P * (u + n)],
-                    lhsT=ident_bf[:],
-                    rhs=rows[:, u : u + n, :, 2 * P * group + e : 2 * P * (group + 1) : 2].rearrange(
-                        "p u f i -> p u i f"
-                    ),
-                    start=True,
-                    stop=True,
-                )
             words = gn[:, r, :].bitcast(F32)
-            for u in range(group, NU):
+            for u in range(first, NU):
                 nc.tensor.transpose(out=t3[:, u, :], in_=words[:, u * P : (u + 1) * P], identity=ident_f[:])
             live["t3", r] = t3
 
         def gn_group(r):
-            gn_g = work.tile([P, G, P, T], BF16, name="gn_g", align_bytes=64)
+            gn_g = live["gn_g", r]
+            first = r // 4
             words = gn_g[:].rearrange("p g i t -> p (g i t)").bitcast(F32).rearrange("p (g i u) -> p g i u", g=G, u=2)
-            nc.scalar.copy(out=words, in_=live["t3", r][:].rearrange("p (g u) i -> p g i u", g=G))
+            nc.scalar.copy(
+                out=words[:, first:G, :, :],
+                in_=live["t3", r][:, 2 * first : NU, :].rearrange("p (g u) i -> p g i u", u=2),
+            )
+
+        def gn_tile(r):
+            gn_g = eight.tile([P, G, P, T], BF16, name="gn_g", align_bytes=64)
             live["gn_g", r] = gn_g
+            if r >= 4:
+                group, e = divmod(r, 2)
+                nc.gpsimd.tensor_scalar(
+                    out=gn_g[:, 0, :, :],
+                    in0=gn[:, 0:4, 2 * P * group + e : 2 * P * (group + 1) : 2].rearrange("p t i -> p i t"),
+                    scalar1=1.0,
+                    scalar2=0.0,
+                    op0=ALU.mult,
+                    op1=ALU.add,
+                )
 
         def gn_quant(b):
             nc.vector.quantize_mx(
@@ -310,13 +314,14 @@ def tile_tls_msc_pb_kernel(tc, h, adj, gcn_bn_g, gcn_bn_b, gcn_w, gcn_b, out):
         setup()
         vec_columns()
         live["sums"] = ps.tile([P, NT], F32, name="sums", tag="ps")
-        for u in range(3):
-            row_sum(2 * u)
-            row_sum(2 * u + 1)
-            column_sums(u)
-            if u == 1:
-                inv_roots(0)
-        column_sums(3)
+        for r in range(NT):
+            with_identity(r)
+        for r in range(4):
+            row_sum(r)
+            column_sums(r)
+        inv_roots(0)
+        for r in range(4, NT):
+            column_sums(r)
         inv_roots(1)
         spread(0)
         spread(1)
@@ -324,6 +329,8 @@ def tile_tls_msc_pb_kernel(tc, h, adj, gcn_bn_g, gcn_bn_b, gcn_w, gcn_b, out):
         for half in range(2):
             for w in range(2):
                 h_turn(w, half)
+        for r in range(4):
+            gn_tile(r)
         scale(0)
         scale(1)
         for w in range(2):
@@ -339,6 +346,7 @@ def tile_tls_msc_pb_kernel(tc, h, adj, gcn_bn_g, gcn_bn_b, gcn_w, gcn_b, out):
             for e in range(2):
                 h_affine(w, 1, e)
         for r in range(4, NT):
+            gn_tile(r)
             scale(r)
         for ct in range(CT):
             hb_turn(ct)

@@ -20,6 +20,7 @@ G = 2
 NU = 4
 T = 4
 NEG_SLOPE = 0.01
+AHEAD = 4
 
 FLOPS = 2 * N * N * D + 2 * N * D * D
 
@@ -68,12 +69,12 @@ def tile_tls_msc_pb_kernel(tc, h, adj, gcn_bn_g, gcn_bn_b, gcn_w, gcn_b, out):
             nc.sync.dma_start(out=vecs[0:2, :], in_=gcn_bn_g.rearrange("(w c) -> w c", w=2))
             nc.sync.dma_start(out=vecs[2:4, :], in_=gcn_bn_b.rearrange("(w c) -> w c", w=2))
             adj_v = adj.rearrange("(u p e) c -> u p e c", u=NU, e=2)
-            for u in range(NU):
-                c = 512 * (u // 2)
-                nc.sync.dma_start(out=adj_sb[:, 2 * u : 2 * u + 2, c:N], in_=adj_v[u, :, :, c:N])
             h_v = h.rearrange("(a p) c -> p a c", p=P)
-            nc.sync.dma_start(out=h_sb[:, 0:4, :], in_=h_v[:, 0:4, :])
-            nc.sync.dma_start(out=h_sb[:, 4:8, :], in_=h_v[:, 4:8, :])
+            for half in range(2):
+                for u in range(2 * half, 2 * half + 2):
+                    c = 512 * half
+                    nc.sync.dma_start(out=adj_sb[:, 2 * u : 2 * u + 2, c:N], in_=adj_v[u, :, :, c:N])
+                nc.sync.dma_start(out=h_sb[:, 4 * half : 4 * half + 4, :], in_=h_v[:, 4 * half : 4 * half + 4, :])
             nc.sync.dma_start(out=w_sb[:].rearrange("p (w e) d -> p w (e d)", e=2), in_=gcn_w.rearrange("(w p e) d -> p w (e d)", p=P, e=2))
             nc.sync.dma_start(out=bias_bc[:], in_=gcn_b.partition_broadcast(P))
             make_identity(nc, ident_bf[:])
@@ -107,24 +108,31 @@ def tile_tls_msc_pb_kernel(tc, h, adj, gcn_bn_g, gcn_bn_b, gcn_w, gcn_b, out):
                 op=ALU.add,
             )
 
-        def column_sums(r):
-            u, e = divmod(r, 2)
-            last = 4 * (r // 4) + 3
-            for a in range(last + 1):
-                nc.tensor.matmul(
-                    out=live["sums"][:, r : r + 1],
-                    lhsT=adj_sb[:, a, 2 * P * u + e : 2 * P * (u + 1) : 2],
-                    rhs=ones[:],
-                    start=(a == 0),
-                    stop=(a == last),
-                )
+        def column_sums(part):
+            first = 4 * (part // 2)
+            for r in range(4 * ((part + 1) // 2), 4 * ((part + 1) // 2) + 4):
+                u, e = divmod(r, 2)
+                c = 4 * part + r % 4
+                for a in range(first, first + 4):
+                    nc.tensor.matmul(
+                        out=live["sums"][:, c : c + 1],
+                        lhsT=adj_sb[:, a, 2 * P * u + e : 2 * P * (u + 1) : 2],
+                        rhs=ones[:],
+                        start=(a == first),
+                        stop=(a == first + 3),
+                    )
 
-        def inv_roots(q):
-            c = slice(4 * q, 4 * q + 4)
-            if q == 0:
+        def inv_roots(half):
+            c = slice(4 * half, 4 * half + 4)
+            if half == 0:
                 nc.vector.tensor_tensor(out=deg[:, c], in0=live["sums"][:, c], in1=row_part[:], op=ALU.add)
             else:
-                nc.vector.tensor_copy(out=deg[:, c], in_=live["sums"][:, c])
+                nc.vector.tensor_reduce(
+                    out=deg[:, c],
+                    in_=live["sums"][:, 4:12].rearrange("p (k r) -> p r k", k=2),
+                    axis=mybir.AxisListType.X,
+                    op=ALU.add,
+                )
             nc.scalar.activation(out=dinv[:, c], in_=deg[:, c], func=ACT.Abs_reciprocal_sqrt, bias=1.0)
 
         def spread(q):
@@ -137,10 +145,10 @@ def tile_tls_msc_pb_kernel(tc, h, adj, gcn_bn_g, gcn_bn_b, gcn_w, gcn_b, out):
                     identity=ident_f[:],
                 )
 
-        def scale(r):
-            half = 512 * (r // 4)
+        def scale(r, half):
+            start = 512 * half
             diag = 2 * P * (r // 2)
-            cuts = sorted(set([half, diag, diag + 2 * P, half + 512, N]))
+            cuts = sorted(set([start, start + 512] + [x for x in (diag, diag + 2 * P) if x // 512 == half]))
             for lo, hi in zip(cuts[:-1], cuts[1:]):
                 src = gd[:, r, :] if lo == diag else adj_sb[:, r, lo:hi]
                 bank = dbc[lo // 512][:, lo % 512 : lo % 512 + hi - lo]
@@ -163,24 +171,14 @@ def tile_tls_msc_pb_kernel(tc, h, adj, gcn_bn_g, gcn_bn_b, gcn_w, gcn_b, out):
                 )
             live["t1", w, half] = t1
 
-        def h_affine(w, half, e):
+        def h_affine(w, half):
             src = live["t1", w, half][:].rearrange("p a n -> p (a n)").bitcast(BF16)
-            src = src.rearrange("p (n e) -> p e n", e=2)[:, e, :]
-            dst = hbt[:, w, e, 512 * half : 512 * (half + 1)]
-            c = 2 * w + e
-            if (w, half) == (1, 1):
-                nc.vector.tensor_scalar(
-                    out=dst,
-                    in0=src,
-                    scalar1=gb[:, c : c + 1],
-                    scalar2=gb[:, CT + c : CT + c + 1],
-                    op0=ALU.mult,
-                    op1=ALU.add,
-                )
-            else:
+            src = src.rearrange("p (n e) -> p e n", e=2)
+            for e in range(2):
+                c = 2 * w + e
                 nc.scalar.activation(
-                    out=dst,
-                    in_=src,
+                    out=hbt[:, w, e, 512 * half : 512 * (half + 1)],
+                    in_=src[:, e, :],
                     func=ACT.Identity,
                     scale=gb[:, c : c + 1],
                     bias=gb[:, CT + c : CT + c + 1],
@@ -271,13 +269,13 @@ def tile_tls_msc_pb_kernel(tc, h, adj, gcn_bn_g, gcn_bn_b, gcn_w, gcn_b, out):
             live["m1", b] = m1
 
         def agg_group(b):
-            ag_g = work.tile([P, P, T], BF16, name="ag_g", align_bytes=64)
+            ag_g = eight.tile([P, P, T], BF16, name="ag_g", align_bytes=64)
             nc.scalar.copy(out=ag_g[:], in_=live["m1", b][:].rearrange("p t i -> p i t"))
             live["ag_g", b] = ag_g
 
         def agg_quant(b):
-            ag_q = work.tile([P, P], U32, name="ag_q", align_bytes=64)
-            ag_s = work.tile([P, P], U8, name="ag_s", align_bytes=64)
+            ag_q = eight.tile([P, P], U32, name="ag_q", align_bytes=64)
+            ag_s = eight.tile([P, P], U8, name="ag_s", align_bytes=64)
             nc.vector.quantize_mx(
                 out=ag_q[:].bitcast(FP8X4), scales=ag_s[:], in_=live["ag_g", b][:].rearrange("p i t -> p (i t)")
             )
@@ -285,7 +283,7 @@ def tile_tls_msc_pb_kernel(tc, h, adj, gcn_bn_g, gcn_bn_b, gcn_w, gcn_b, out):
 
         def second_matmul(b):
             ag_q, ag_s = live["ag_q", b]
-            m2 = ps.tile([P, D], F32, name="m2", tag="ps")
+            m2 = ps_c.tile([P, D], F32, name="m2", tag="dbc%d" % (b % 2))
             nc.tensor.matmul_mx(
                 out=m2[:],
                 lhsT=ag_q[:].bitcast(FP8X4),
@@ -313,71 +311,58 @@ def tile_tls_msc_pb_kernel(tc, h, adj, gcn_bn_g, gcn_bn_b, gcn_w, gcn_b, out):
 
         setup()
         vec_columns()
-        live["sums"] = ps.tile([P, NT], F32, name="sums", tag="ps")
+        live["sums"] = ps.tile([P, 12], F32, name="sums", tag="ps")
         for r in range(NT):
             with_identity(r)
         for r in range(4):
-            row_sum(r)
-            column_sums(r)
-        inv_roots(0)
-        for r in range(4, NT):
-            column_sums(r)
-        inv_roots(1)
-        spread(0)
-        spread(1)
-        w_group()
-        for half in range(2):
-            for w in range(2):
-                h_turn(w, half)
+            gn_tile(r)
         for r in range(4):
-            gn_tile(r)
-        scale(0)
-        scale(1)
-        for w in range(2):
-            for e in range(2):
-                h_affine(w, 0, e)
-        gn_turn(0)
-        gn_group(0)
-        scale(2)
-        scale(3)
-        gn_turn(1)
-        gn_group(1)
-        for w in range(2):
-            for e in range(2):
-                h_affine(w, 1, e)
-        for r in range(4, NT):
-            gn_tile(r)
-            scale(r)
+            row_sum(r)
+        column_sums(0)
+        inv_roots(0)
+        column_sums(1)
+        spread(0)
+        h_turn(0, 0)
+        column_sums(2)
+        h_turn(1, 0)
+        h_turn(0, 1)
+        h_affine(0, 0)
+        scale(0, 0)
+        inv_roots(1)
+        for r in range(1, 4):
+            scale(r, 0)
+        spread(1)
+        h_turn(1, 1)
+        h_affine(1, 0)
+        h_affine(0, 1)
+        h_affine(1, 1)
+        w_group()
+        for r in range(4):
+            scale(r, 1)
         for ct in range(CT):
             hb_turn(ct)
             hb_group(ct)
-        gn_quant(0)
-        gn_quant(1)
-        for r in range(2, 6):
-            gn_turn(r)
-            if r < 4:
-                gn_group(r)
+        for r in range(4, NT):
+            gn_tile(r)
+            scale(r, 1)
         hb_quant(0)
         hb_quant(1)
-        gn_quant(2)
-        first_matmul(0)
-        gn_quant(3)
+        for r in range(NT):
+            gn_turn(r)
+            gn_group(r)
+        for r in range(NT):
+            gn_quant(r)
         w_quant()
-        first_matmul(1)
+        for k in range(AHEAD):
+            first_matmul(k)
         for k in range(NT + 2):
             if k < NT:
                 agg_group(k)
-            if k + 4 < NT:
-                gn_group(k + 4)
+            if k + AHEAD < NT:
+                first_matmul(k + AHEAD)
             if k < NT:
                 agg_quant(k)
                 second_matmul(k)
-            if k + 4 < NT:
-                gn_quant(k + 4)
-            if k + 2 < NT:
-                first_matmul(k + 2)
-            if k + 6 < NT:
-                gn_turn(k + 6)
             if 1 <= k <= NT:
                 add_bias(k - 1)
             if k >= 2:

@@ -20,7 +20,7 @@ G = 2
 NU = 4
 T = 4
 NEG_SLOPE = 0.01
-AHEAD = 4
+PAIR = (0, 1)
 
 FLOPS = 2 * N * N * D + 2 * N * D * D
 
@@ -29,7 +29,6 @@ def tile_tls_msc_pb_kernel(tc, h, adj, gcn_bn_g, gcn_bn_b, gcn_w, gcn_b, out):
     nc = tc.nc
     with ExitStack() as ctx:
         keep = ctx.enter_context(tc.tile_pool(name="keep", bufs=1))
-        work = ctx.enter_context(tc.tile_pool(name="work", bufs=4))
         eight = ctx.enter_context(tc.tile_pool(name="eight", bufs=NT))
         ps_c = ctx.enter_context(tc.psum_pool(name="ps_c", bufs=1))
         ps = ctx.enter_context(tc.psum_pool(name="ps", bufs=6))
@@ -43,6 +42,14 @@ def tile_tls_msc_pb_kernel(tc, h, adj, gcn_bn_g, gcn_bn_b, gcn_w, gcn_b, out):
         h_sb = keep.tile([P, NT, D], BF16, name="h_sb")
         w_sb = keep.tile([P, T, D], BF16, name="w_sb")
         bias_bc = keep.tile([P, D], BF16, name="bias_bc")
+        bias_row = keep.tile([P, P], BF16, name="bias_row")
+        bias_hi = keep.tile([P, CT], F32, name="bias_hi")
+        bias_lo = keep.tile([P, CT], F32, name="bias_lo")
+        ag_pair_g = keep.tile([P, 2, P, T], BF16, name="ag_pair_g", align_bytes=64)
+        ag_pair_q = keep.tile([P, 2 * P], U32, name="ag_pair_q", align_bytes=64)
+        ag_pair_s = keep.tile([P, 2 * P], U8, name="ag_pair_s", align_bytes=64)
+        hi = keep.tile([P, CT, 2 * P], F32, name="hi")
+        low = keep.tile([P, CT, 2 * P], F32, name="low")
         ones = keep.tile([P, 1], BF16, name="ones")
         row_part = keep.tile([P, 4], F32, name="row_part")
         junk = keep.tile([P, 512], BF16, name="junk")
@@ -66,19 +73,22 @@ def tile_tls_msc_pb_kernel(tc, h, adj, gcn_bn_g, gcn_bn_b, gcn_w, gcn_b, out):
 
         def setup():
             nc.vector.memset(vecs[:], 0.0)
-            nc.sync.dma_start(out=vecs[0:2, :], in_=gcn_bn_g.rearrange("(w c) -> w c", w=2))
-            nc.sync.dma_start(out=vecs[2:4, :], in_=gcn_bn_b.rearrange("(w c) -> w c", w=2))
             adj_v = adj.rearrange("(u p e) c -> u p e c", u=NU, e=2)
             h_v = h.rearrange("(a p) c -> p a c", p=P)
             for half in range(2):
                 for u in range(2 * half, 2 * half + 2):
                     c = 512 * half
                     nc.sync.dma_start(out=adj_sb[:, 2 * u : 2 * u + 2, c:N], in_=adj_v[u, :, :, c:N])
+                if half == 0:
+                    nc.sync.dma_start(out=vecs[0:2, :], in_=gcn_bn_g.rearrange("(w c) -> w c", w=2))
+                    nc.sync.dma_start(out=vecs[2:4, :], in_=gcn_bn_b.rearrange("(w c) -> w c", w=2))
                 nc.sync.dma_start(out=h_sb[:, 4 * half : 4 * half + 4, :], in_=h_v[:, 4 * half : 4 * half + 4, :])
             nc.sync.dma_start(out=w_sb[:].rearrange("p (w e) d -> p w (e d)", e=2), in_=gcn_w.rearrange("(w p e) d -> p w (e d)", p=P, e=2))
             nc.sync.dma_start(out=bias_bc[:], in_=gcn_b.partition_broadcast(P))
             make_identity(nc, ident_bf[:])
             make_identity(nc, ident_f[:])
+            nc.vector.memset(bias_row[:], 0.0)
+            nc.sync.dma_start(out=bias_row[0:CT, :], in_=gcn_b.rearrange("(t p) -> t p", p=P))
             nc.vector.memset(warm[:], 1.0)
             nc.vector.memset(ones[:], 1.0)
             nc.vector.memset(ident_2[:], 0.0)
@@ -90,6 +100,12 @@ def tile_tls_msc_pb_kernel(tc, h, adj, gcn_bn_g, gcn_bn_b, gcn_w, gcn_b, out):
             tv = ps.tile([P, P], F32, name="tv", tag="ps")
             nc.tensor.transpose(out=tv[:], in_=vecs[:].bitcast(F32), identity=ident_f[:])
             nc.vector.tensor_copy(out=gb[:], in_=tv[:].bitcast(BF16)[:, 0:8])
+
+        def bias_columns():
+            tb = ps.tile([P, P], BF16, name="tb", tag="ps")
+            nc.tensor.transpose(out=tb[:], in_=bias_row[:], identity=ident_bf[:])
+            nc.scalar.activation(out=bias_hi[:], in_=tb[:, 0:CT], func=ACT.Copy, scale=1.0 - NEG_SLOPE)
+            nc.scalar.activation(out=bias_lo[:], in_=tb[:, 0:CT], func=ACT.Copy, scale=NEG_SLOPE)
 
         def row_sum(r):
             right = adj_sb[:, r, 512:N]
@@ -269,15 +285,18 @@ def tile_tls_msc_pb_kernel(tc, h, adj, gcn_bn_g, gcn_bn_b, gcn_w, gcn_b, out):
             live["m1", b] = m1
 
         def agg_group(b):
-            ag_g = eight.tile([P, P, T], BF16, name="ag_g", align_bytes=64)
-            nc.scalar.copy(out=ag_g[:], in_=live["m1", b][:].rearrange("p t i -> p i t"))
+            if b in PAIR:
+                ag_g = ag_pair_g[:, b, :, :]
+            else:
+                ag_g = eight.tile([P, P, T], BF16, name="ag_g", align_bytes=64)[:]
+            nc.scalar.copy(out=ag_g, in_=live["m1", b][:].rearrange("p t i -> p i t"))
             live["ag_g", b] = ag_g
 
         def agg_quant(b):
             ag_q = eight.tile([P, P], U32, name="ag_q", align_bytes=64)
             ag_s = eight.tile([P, P], U8, name="ag_s", align_bytes=64)
             nc.vector.quantize_mx(
-                out=ag_q[:].bitcast(FP8X4), scales=ag_s[:], in_=live["ag_g", b][:].rearrange("p i t -> p (i t)")
+                out=ag_q[:].bitcast(FP8X4), scales=ag_s[:], in_=live["ag_g", b].rearrange("p i t -> p (i t)")
             )
             live["ag_q", b] = (ag_q, ag_s)
 
@@ -295,22 +314,77 @@ def tile_tls_msc_pb_kernel(tc, h, adj, gcn_bn_g, gcn_bn_b, gcn_w, gcn_b, out):
             )
             live["m2", b] = m2
 
+        def pair_quant():
+            nc.vector.quantize_mx(
+                out=ag_pair_q[:].bitcast(FP8X4),
+                scales=ag_pair_s[:],
+                in_=ag_pair_g[:].rearrange("p b i t -> p (b i t)"),
+            )
+
+        def pair_matmul():
+            for j in range(2):
+                m2 = ps.tile([P, 2, 2 * P], F32, name="m2t", tag="ps")
+                for c in range(2):
+                    ct = 2 * j + c
+                    nc.tensor.matmul_mx(
+                        out=m2[:, c, :],
+                        lhsT=w_q[:, ct * P : (ct + 1) * P].bitcast(FP8X4),
+                        lhsT_scale=w_s[:, ct * P : (ct + 1) * P],
+                        rhs=ag_pair_q[:].bitcast(FP8X4),
+                        rhs_scale=ag_pair_s[:],
+                        start=True,
+                        stop=True,
+                    )
+                live["m2t", j] = m2
+
+        def pair_leaky(j):
+            for c in range(2):
+                ct = 2 * j + c
+                src = live["m2t", j][:, c, :]
+                nc.scalar.activation(
+                    out=hi[:, ct, :], in_=src, func=ACT.Relu, scale=1.0 - NEG_SLOPE, bias=bias_hi[:, ct : ct + 1]
+                )
+                nc.scalar.activation(
+                    out=low[:, ct, :], in_=src, func=ACT.Identity, scale=NEG_SLOPE, bias=bias_lo[:, ct : ct + 1]
+                )
+
+        def pair_turn(h):
+            n = ps.tile([P, CT, P], F32, name="n", tag="ps")
+            for ct in range(CT):
+                for part, first in ((hi, True), (low, False)):
+                    nc.tensor.matmul(
+                        out=n[:, ct, :],
+                        lhsT=part[:, ct, h * P : (h + 1) * P],
+                        rhs=ident_f[:],
+                        is_transpose=True,
+                        start=first,
+                        stop=not first,
+                    )
+            live["n", h] = n
+
+        def pair_store(h):
+            res = eight.tile([P, D], F32, name="res")
+            nc.scalar.copy(out=res[:], in_=live["n", h][:].rearrange("p c d -> p (c d)"))
+            store(h, res)
+
+        def store(b, res):
+            out_v = out.rearrange("(u p e) d -> u e p d", u=NU, e=2)
+            nc.sync.dma_start(out=out_v[b // 2, b % 2], in_=res[:])
+
         def add_bias(b):
-            lin = work.tile([P, D], F32, name="lin")
+            lin = eight.tile([P, D], F32, name="lin")
             nc.vector.tensor_tensor(out=lin[:], in0=live["m2", b][:], in1=bias_bc[:], op=ALU.add)
             live["lin", b] = lin
 
         def leaky(b):
             lin = live["lin", b]
-            res = work.tile([P, D], F32, name="res")
+            res = eight.tile([P, D], F32, name="res")
             nc.vector.scalar_tensor_tensor(
                 out=res[:], in0=lin[:], scalar=NEG_SLOPE, in1=lin[:], op0=ALU.mult, op1=ALU.max
             )
-            out_v = out.rearrange("(u p e) d -> u e p d", u=NU, e=2)
-            nc.sync.dma_start(out=out_v[b // 2, b % 2], in_=res[:])
+            store(b, res)
 
         setup()
-        vec_columns()
         live["sums"] = ps.tile([P, 12], F32, name="sums", tag="ps")
         for r in range(NT):
             with_identity(r)
@@ -321,6 +395,7 @@ def tile_tls_msc_pb_kernel(tc, h, adj, gcn_bn_g, gcn_bn_b, gcn_w, gcn_b, out):
         column_sums(0)
         inv_roots(0)
         column_sums(1)
+        vec_columns()
         spread(0)
         h_turn(0, 0)
         column_sums(2)
@@ -350,20 +425,34 @@ def tile_tls_msc_pb_kernel(tc, h, adj, gcn_bn_g, gcn_bn_b, gcn_w, gcn_b, out):
         for r in range(NT):
             gn_turn(r)
             gn_group(r)
-        for r in range(NT):
+        bias_columns()
+        for r in range(5):
             gn_quant(r)
+            first_matmul(r)
+        gn_quant(5)
         w_quant()
-        for k in range(AHEAD):
-            first_matmul(k)
-        for k in range(NT + 2):
+        agg_group(0)
+        agg_group(1)
+        pair_quant()
+        pair_matmul()
+        for k in range(2, NT + 2):
             if k < NT:
                 agg_group(k)
-            if k + AHEAD < NT:
-                first_matmul(k + AHEAD)
-            if k < NT:
                 agg_quant(k)
                 second_matmul(k)
-            if 1 <= k <= NT:
+            if k + 3 < NT:
+                first_matmul(k + 3)
+            if k == 2:
+                gn_quant(6)
+                gn_quant(7)
+            if k in (4, 5):
+                pair_leaky(k - 4)
+            if k == 6:
+                pair_turn(0)
+                pair_turn(1)
+            if k in (7, 8):
+                pair_store(k - 7)
+            if 2 <= k - 1 < NT:
                 add_bias(k - 1)
-            if k >= 2:
+            if k >= 4:
                 leaky(k - 2)

@@ -36,13 +36,12 @@ def tile_tls_msc_pb_kernel(tc, h, adj, gcn_bn_g, gcn_bn_b, gcn_w, gcn_b, out):
 
         ident_bf = keep.tile([P, P], BF16, name="ident_bf")
         ident_f = keep.tile([P, P], F32, name="ident_f")
-        vecs = keep.tile([P, 2 * P], BF16, name="vecs")
+        vecs = keep.tile([P, P], BF16, name="vecs")
         warm = keep.tile([P, 1], F32, name="warm")
         adj_sb = keep.tile([P, NT, N], BF16, name="adj_sb")
         h_sb = keep.tile([P, NT, D], BF16, name="h_sb")
         w_sb = keep.tile([P, T, D], BF16, name="w_sb")
         bias_bc = keep.tile([P, D], BF16, name="bias_bc")
-        bias_row = keep.tile([P, P], BF16, name="bias_row")
         bias_hi = keep.tile([P, CT], F32, name="bias_hi")
         bias_lo = keep.tile([P, CT], F32, name="bias_lo")
         ag_pair_g = keep.tile([P, 2, P, T], BF16, name="ag_pair_g", align_bytes=64)
@@ -57,8 +56,8 @@ def tile_tls_msc_pb_kernel(tc, h, adj, gcn_bn_g, gcn_bn_b, gcn_w, gcn_b, out):
         gd = keep.tile([P, NT, 2 * P], F32, name="gd")
         ident_2 = keep.tile([P, 2, P, 2], F32, name="ident_2")
         dinv = keep.tile([P, NT], F32, name="dinv")
-        gb = keep.tile([P, 2 * CT], F32, name="gb")
-        hbt = keep.tile([P, 2, 2, N], BF16, name="hbt")
+        gb = keep.tile([P, 3 * CT], F32, name="gb")
+        hbt = keep.tile([P, CT, N], BF16, name="hbt")
         hb_g = keep.tile([P, G, D, T], BF16, name="hb_g", align_bytes=64)
         hb_q = keep.tile([P, G, D], U32, name="hb_q", align_bytes=64)
         hb_s = keep.tile([P, G, D], U8, name="hb_s", align_bytes=64)
@@ -80,15 +79,13 @@ def tile_tls_msc_pb_kernel(tc, h, adj, gcn_bn_g, gcn_bn_b, gcn_w, gcn_b, out):
                     c = 512 * half
                     nc.sync.dma_start(out=adj_sb[:, 2 * u : 2 * u + 2, c:N], in_=adj_v[u, :, :, c:N])
                 if half == 0:
-                    nc.sync.dma_start(out=vecs[0:2, :], in_=gcn_bn_g.rearrange("(w c) -> w c", w=2))
-                    nc.sync.dma_start(out=vecs[2:4, :], in_=gcn_bn_b.rearrange("(w c) -> w c", w=2))
+                    for k, v in enumerate((gcn_bn_g, gcn_bn_b, gcn_b)):
+                        nc.sync.dma_start(out=vecs[k * CT : (k + 1) * CT, :], in_=v.rearrange("(t p) -> t p", p=P))
                 nc.sync.dma_start(out=h_sb[:, 4 * half : 4 * half + 4, :], in_=h_v[:, 4 * half : 4 * half + 4, :])
-            nc.sync.dma_start(out=w_sb[:].rearrange("p (w e) d -> p w (e d)", e=2), in_=gcn_w.rearrange("(w p e) d -> p w (e d)", p=P, e=2))
+            nc.sync.dma_start(out=w_sb[:], in_=gcn_w.rearrange("(t p) d -> p t d", p=P))
             nc.sync.dma_start(out=bias_bc[:], in_=gcn_b.partition_broadcast(P))
             make_identity(nc, ident_bf[:])
             make_identity(nc, ident_f[:])
-            nc.vector.memset(bias_row[:], 0.0)
-            nc.sync.dma_start(out=bias_row[0:CT, :], in_=gcn_b.rearrange("(t p) -> t p", p=P))
             nc.vector.memset(warm[:], 1.0)
             nc.vector.memset(ones[:], 1.0)
             nc.vector.memset(ident_2[:], 0.0)
@@ -97,15 +94,16 @@ def tile_tls_msc_pb_kernel(tc, h, adj, gcn_bn_g, gcn_bn_b, gcn_w, gcn_b, out):
             nc.scalar.activation(out=warm[:], in_=warm[:], func=ACT.Abs_reciprocal_sqrt)
 
         def vec_columns():
-            tv = ps.tile([P, P], F32, name="tv", tag="ps")
-            nc.tensor.transpose(out=tv[:], in_=vecs[:].bitcast(F32), identity=ident_f[:])
-            nc.vector.tensor_copy(out=gb[:], in_=tv[:].bitcast(BF16)[:, 0:8])
+            tv = ps.tile([P, P], BF16, name="tv", tag="ps")
+            nc.tensor.transpose(out=tv[:], in_=vecs[:], identity=ident_bf[:])
+            live["tv"] = tv
+
+        def vec_copy():
+            nc.scalar.copy(out=gb[:], in_=live["tv"][:, 0 : 3 * CT])
 
         def bias_columns():
-            tb = ps.tile([P, P], BF16, name="tb", tag="ps")
-            nc.tensor.transpose(out=tb[:], in_=bias_row[:], identity=ident_bf[:])
-            nc.scalar.activation(out=bias_hi[:], in_=tb[:, 0:CT], func=ACT.Copy, scale=1.0 - NEG_SLOPE)
-            nc.scalar.activation(out=bias_lo[:], in_=tb[:, 0:CT], func=ACT.Copy, scale=NEG_SLOPE)
+            nc.scalar.activation(out=bias_hi[:], in_=gb[:, 2 * CT : 3 * CT], func=ACT.Copy, scale=1.0 - NEG_SLOPE)
+            nc.scalar.activation(out=bias_lo[:], in_=gb[:, 2 * CT : 3 * CT], func=ACT.Copy, scale=NEG_SLOPE)
 
         def row_sum(r):
             right = adj_sb[:, r, 512:N]
@@ -124,14 +122,13 @@ def tile_tls_msc_pb_kernel(tc, h, adj, gcn_bn_g, gcn_bn_b, gcn_w, gcn_b, out):
                 op=ALU.add,
             )
 
-        def column_sums(part):
-            first = 4 * (part // 2)
-            for r in range(4 * ((part + 1) // 2), 4 * ((part + 1) // 2) + 4):
+        def column_sums(half, first):
+            for r in range(4 * half, 4 * half + 4):
                 u, e = divmod(r, 2)
-                c = 4 * part + r % 4
+                c = first + r % 4 if half else r
                 for a in range(first, first + 4):
                     nc.tensor.matmul(
-                        out=live["sums"][:, c : c + 1],
+                        out=live["sums", half][:, c : c + 1],
                         lhsT=adj_sb[:, a, 2 * P * u + e : 2 * P * (u + 1) : 2],
                         rhs=ones[:],
                         start=(a == first),
@@ -140,12 +137,13 @@ def tile_tls_msc_pb_kernel(tc, h, adj, gcn_bn_g, gcn_bn_b, gcn_w, gcn_b, out):
 
         def inv_roots(half):
             c = slice(4 * half, 4 * half + 4)
+            sums = live["sums", half]
             if half == 0:
-                nc.vector.tensor_tensor(out=deg[:, c], in0=live["sums"][:, c], in1=row_part[:], op=ALU.add)
+                nc.vector.tensor_tensor(out=deg[:, c], in0=sums[:], in1=row_part[:], op=ALU.add)
             else:
                 nc.vector.tensor_reduce(
                     out=deg[:, c],
-                    in_=live["sums"][:, 4:12].rearrange("p (k r) -> p r k", k=2),
+                    in_=sums[:].rearrange("p (k r) -> p r k", k=2),
                     axis=mybir.AxisListType.X,
                     op=ALU.add,
                 )
@@ -177,32 +175,30 @@ def tile_tls_msc_pb_kernel(tc, h, adj, gcn_bn_g, gcn_bn_b, gcn_w, gcn_b, out):
                     op1=ALU.mult,
                 )
 
-        def h_turn(w, half):
+        def h_turn(ct, half):
             t1 = ps.tile([P, 4, P], F32, name="t1", tag="ps")
             for a in range(4):
-                nc.tensor.transpose(
+                nc.tensor.matmul(
                     out=t1[:, a, :],
-                    in_=h_sb[:, 4 * half + a, :].bitcast(F32)[:, w * P : (w + 1) * P],
-                    identity=ident_f[:],
+                    lhsT=h_sb[:, 4 * half + a, ct * P : (ct + 1) * P],
+                    rhs=ident_bf[:],
+                    start=True,
+                    stop=True,
                 )
-            live["t1", w, half] = t1
+            live["t1", ct, half] = t1
 
-        def h_affine(w, half):
-            src = live["t1", w, half][:].rearrange("p a n -> p (a n)").bitcast(BF16)
-            src = src.rearrange("p (n e) -> p e n", e=2)
-            for e in range(2):
-                c = 2 * w + e
-                nc.scalar.activation(
-                    out=hbt[:, w, e, 512 * half : 512 * (half + 1)],
-                    in_=src[:, e, :],
-                    func=ACT.Identity,
-                    scale=gb[:, c : c + 1],
-                    bias=gb[:, CT + c : CT + c + 1],
-                )
+        def h_affine(ct, half):
+            nc.scalar.activation(
+                out=hbt[:, ct, 512 * half : 512 * (half + 1)],
+                in_=live["t1", ct, half][:].rearrange("p a n -> p (a n)"),
+                func=ACT.Identity,
+                scale=gb[:, ct : ct + 1],
+                bias=gb[:, CT + ct : CT + ct + 1],
+            )
 
         def hb_turn(ct):
             t2 = ps.tile([P, NU, P], F32, name="t2", tag="ps")
-            words = hbt[:, ct // 2, ct % 2, :].bitcast(F32)
+            words = hbt[:, ct, :].bitcast(F32)
             for u in range(NU):
                 nc.tensor.transpose(out=t2[:, u, :], in_=words[:, u * P : (u + 1) * P], identity=ident_f[:])
             live["t2", ct] = t2
@@ -385,32 +381,36 @@ def tile_tls_msc_pb_kernel(tc, h, adj, gcn_bn_g, gcn_bn_b, gcn_w, gcn_b, out):
             store(b, res)
 
         setup()
-        live["sums"] = ps.tile([P, 12], F32, name="sums", tag="ps")
+        live["sums", 0] = ps.tile([P, 4], F32, name="sums_a", tag="ps")
+        live["sums", 1] = ps.tile([P, 8], F32, name="sums_b", tag="ps")
         for r in range(NT):
             with_identity(r)
         for r in range(4):
             gn_tile(r)
         for r in range(4):
             row_sum(r)
-        column_sums(0)
+        column_sums(0, 0)
         inv_roots(0)
-        column_sums(1)
-        vec_columns()
+        column_sums(1, 0)
         spread(0)
-        h_turn(0, 0)
-        column_sums(2)
-        h_turn(1, 0)
-        h_turn(0, 1)
-        h_affine(0, 0)
+        vec_columns()
+        vec_copy()
+        for ct in range(2):
+            h_turn(ct, 0)
+            h_affine(ct, 0)
         scale(0, 0)
+        column_sums(1, 4)
+        scale(1, 0)
         inv_roots(1)
-        for r in range(1, 4):
-            scale(r, 0)
+        for ct in range(2, CT):
+            h_turn(ct, 0)
+            h_affine(ct, 0)
         spread(1)
-        h_turn(1, 1)
-        h_affine(1, 0)
-        h_affine(0, 1)
-        h_affine(1, 1)
+        scale(2, 0)
+        scale(3, 0)
+        for ct in range(CT):
+            h_turn(ct, 1)
+            h_affine(ct, 1)
         w_group()
         for r in range(4):
             scale(r, 1)

@@ -51,7 +51,7 @@ def tile_tls_msc_pb_kernel(tc, h, adj, gcn_bn_g, gcn_bn_b, gcn_w, gcn_b, out):
         low = keep.tile([P, CT, 2 * P], F32, name="low")
         ones = keep.tile([P, 1], BF16, name="ones")
         row_part = keep.tile([P, 4], F32, name="row_part")
-        junk = keep.tile([P, 512], BF16, name="junk")
+        junk = keep.tile([P, N], BF16, name="junk")
         deg = keep.tile([P, NT], F32, name="deg")
         gd = keep.tile([P, NT, 2 * P], F32, name="gd")
         ident_2 = keep.tile([P, 2, P, 2], F32, name="ident_2")
@@ -106,12 +106,12 @@ def tile_tls_msc_pb_kernel(tc, h, adj, gcn_bn_g, gcn_bn_b, gcn_w, gcn_b, out):
             nc.scalar.activation(out=bias_lo[:], in_=gb[:, 2 * CT : 3 * CT], func=ACT.Copy, scale=NEG_SLOPE)
 
         def row_sum(r):
-            right = adj_sb[:, r, 512:N]
+            right = adj_sb[:, r, 512 * (r // 2) : N]
             part = row_part[:, r : r + 1]
             if r % 2 == 0:
                 nc.vector.tensor_reduce(out=part, in_=right, axis=mybir.AxisListType.X, op=ALU.add)
             else:
-                nc.scalar.activation(out=junk[:], in_=right, func=ACT.Copy, accum_out=part)
+                nc.scalar.activation(out=junk[:, 512 * (r // 2) : N], in_=right, func=ACT.Copy, accum_out=part)
 
         def with_identity(r):
             u, e = divmod(r, 2)
@@ -122,58 +122,40 @@ def tile_tls_msc_pb_kernel(tc, h, adj, gcn_bn_g, gcn_bn_b, gcn_w, gcn_b, out):
                 op=ALU.add,
             )
 
-        def column_sums(half, first):
-            for r in range(4 * half, 4 * half + 4):
+        def column_sums(sums, rows, first):
+            for k, r in enumerate(rows):
                 u, e = divmod(r, 2)
-                c = first + r % 4 if half else r
                 for a in range(first, first + 4):
                     nc.tensor.matmul(
-                        out=live["sums", half][:, c : c + 1],
+                        out=sums[:, k : k + 1],
                         lhsT=adj_sb[:, a, 2 * P * u + e : 2 * P * (u + 1) : 2],
                         rhs=ones[:],
                         start=(a == first),
                         stop=(a == first + 3),
                     )
 
-        def inv_roots(half):
-            c = slice(4 * half, 4 * half + 4)
-            sums = live["sums", half]
-            if half == 0:
-                nc.vector.tensor_tensor(out=deg[:, c], in0=sums[:], in1=row_part[:], op=ALU.add)
-            else:
-                nc.vector.tensor_reduce(
-                    out=deg[:, c],
-                    in_=sums[:].rearrange("p (k r) -> p r k", k=2),
-                    axis=mybir.AxisListType.X,
-                    op=ALU.add,
-                )
-            nc.scalar.activation(out=dinv[:, c], in_=deg[:, c], func=ACT.Abs_reciprocal_sqrt, bias=1.0)
+        def inv_roots(c, total):
+            nc.scalar.activation(out=dinv[:, c], in_=total, func=ACT.Abs_reciprocal_sqrt, bias=1.0)
 
-        def spread(q):
-            for r in range(4):
-                c = 4 * q + r
-                first = 2 * P * (r // 2) + r % 2
+        def spread(u):
+            for e in range(2):
+                c = 2 * u + e
                 nc.tensor.transpose(
-                    out=dbc[q][:, first : 2 * P * (r // 2 + 1) : 2],
+                    out=roots[u][:, e : 2 * P : 2],
                     in_=dinv[:, c : c + 1].to_broadcast([P, P]),
                     identity=ident_f[:],
                 )
 
-        def scale(r, half):
-            start = 512 * half
-            diag = 2 * P * (r // 2)
-            cuts = sorted(set([start, start + 512] + [x for x in (diag, diag + 2 * P) if x // 512 == half]))
-            for lo, hi in zip(cuts[:-1], cuts[1:]):
-                src = gd[:, r, :] if lo == diag else adj_sb[:, r, lo:hi]
-                bank = dbc[lo // 512][:, lo % 512 : lo % 512 + hi - lo]
-                nc.vector.scalar_tensor_tensor(
-                    out=gn[:, r, lo:hi],
-                    in0=src,
-                    scalar=dinv[:, r : r + 1],
-                    in1=bank,
-                    op0=ALU.mult,
-                    op1=ALU.mult,
-                )
+        def scale(r, lo, hi):
+            on_diagonal = (lo, hi) == (2 * P * (r // 2), 2 * P * (r // 2 + 1))
+            nc.vector.scalar_tensor_tensor(
+                out=gn[:, r, lo:hi],
+                in0=gd[:, r, :] if on_diagonal else adj_sb[:, r, lo:hi],
+                scalar=dinv[:, r : r + 1],
+                in1=roots[lo // (2 * P)][:, 0 : hi - lo],
+                op0=ALU.mult,
+                op1=ALU.mult,
+            )
 
         def h_turn(ct, half):
             t1 = ps.tile([P, 4, P], F32, name="t1", tag="ps")
@@ -187,14 +169,15 @@ def tile_tls_msc_pb_kernel(tc, h, adj, gcn_bn_g, gcn_bn_b, gcn_w, gcn_b, out):
                 )
             live["t1", ct, half] = t1
 
-        def h_affine(ct, half):
-            nc.scalar.activation(
-                out=hbt[:, ct, 512 * half : 512 * (half + 1)],
-                in_=live["t1", ct, half][:].rearrange("p a n -> p (a n)"),
-                func=ACT.Identity,
-                scale=gb[:, ct : ct + 1],
-                bias=gb[:, CT + ct : CT + ct + 1],
-            )
+        def h_affine(ct, half, vector=False):
+            dst = hbt[:, ct, 512 * half : 512 * (half + 1)]
+            src = live["t1", ct, half][:].rearrange("p a n -> p (a n)")
+            gain = gb[:, ct : ct + 1]
+            shift = gb[:, CT + ct : CT + ct + 1]
+            if vector:
+                nc.vector.tensor_scalar(out=dst, in0=src, scalar1=gain, scalar2=shift, op0=ALU.mult, op1=ALU.add)
+            else:
+                nc.scalar.activation(out=dst, in_=src, func=ACT.Identity, scale=gain, bias=shift)
 
         def hb_turn(ct):
             t2 = ps.tile([P, NU, P], F32, name="t2", tag="ps")
@@ -381,45 +364,64 @@ def tile_tls_msc_pb_kernel(tc, h, adj, gcn_bn_g, gcn_bn_b, gcn_w, gcn_b, out):
             store(b, res)
 
         setup()
-        live["sums", 0] = ps.tile([P, 4], F32, name="sums_a", tag="ps")
-        live["sums", 1] = ps.tile([P, 8], F32, name="sums_b", tag="ps")
+        first_roots = ps.tile([P, 2 * P], F32, name="first_roots", tag="ps")
+        roots = [first_roots[:], dbc[0][:, 0 : 2 * P], dbc[1][:], dbc[1][:, 2 * P : 4 * P]]
+        sums_1 = ps.tile([P, 2], F32, name="sums_1", tag="ps")
+        sums_2 = ps.tile([P, 2, 4], F32, name="sums_2", tag="ps")
         for r in range(NT):
             with_identity(r)
         for r in range(4):
             gn_tile(r)
-        for r in range(4):
-            row_sum(r)
-        column_sums(0, 0)
-        inv_roots(0)
-        column_sums(1, 0)
+        row_sum(0)
+        row_sum(1)
+        inv_roots(slice(0, 2), row_part[:, 0:2])
+        row_sum(2)
+        row_sum(3)
+        column_sums(sums_1[:], (2, 3), 0)
+        nc.vector.tensor_tensor(out=deg[:, 2:4], in0=sums_1[:], in1=row_part[:, 2:4], op=ALU.add)
+        inv_roots(slice(2, 4), deg[:, 2:4])
         spread(0)
+        column_sums(sums_2[:, 0, :], range(4, NT), 0)
         vec_columns()
         vec_copy()
-        for ct in range(2):
-            h_turn(ct, 0)
-            h_affine(ct, 0)
-        scale(0, 0)
-        column_sums(1, 4)
-        scale(1, 0)
-        inv_roots(1)
+        h_turn(0, 0)
+        h_affine(0, 0)
+        for r in range(4):
+            scale(r, 0, 2 * P)
+        spread(1)
+        h_turn(1, 0)
+        h_affine(1, 0)
+        for r in range(2):
+            scale(r, 2 * P, 4 * P)
+        column_sums(sums_2[:, 1, :], range(4, NT), 4)
+        nc.vector.tensor_reduce(
+            out=deg[:, 4:8], in_=sums_2[:].rearrange("p k r -> p r k"), axis=mybir.AxisListType.X, op=ALU.add
+        )
+        inv_roots(slice(4, 8), deg[:, 4:8])
+        for r in range(2, 4):
+            scale(r, 2 * P, 4 * P)
         for ct in range(2, CT):
             h_turn(ct, 0)
-            h_affine(ct, 0)
-        spread(1)
-        scale(2, 0)
-        scale(3, 0)
+            h_affine(ct, 0, vector=(ct == 2))
+        spread(2)
+        spread(3)
         for ct in range(CT):
             h_turn(ct, 1)
+        for ct in range(CT - 1):
             h_affine(ct, 1)
         w_group()
-        for r in range(4):
-            scale(r, 1)
+        for r in range(2):
+            scale(r, 512, N)
+        h_affine(CT - 1, 1, vector=True)
+        for r in range(2, 4):
+            scale(r, 512, N)
         for ct in range(CT):
             hb_turn(ct)
             hb_group(ct)
         for r in range(4, NT):
             gn_tile(r)
-            scale(r, 1)
+            scale(r, 512, 512 + 2 * P)
+            scale(r, 512 + 2 * P, N)
         hb_quant(0)
         hb_quant(1)
         for r in range(NT):

@@ -20,6 +20,7 @@ G = 2
 NU = 4
 T = 4
 NEG_SLOPE = 0.01
+VECTOR_PIECES = ((2, 0), (CT - 1, 1))
 PAIR = (0, 1)
 
 FLOPS = 2 * N * N * D + 2 * N * D * D
@@ -158,23 +159,22 @@ def tile_tls_msc_pb_kernel(tc, h, adj, gcn_bn_g, gcn_bn_b, gcn_w, gcn_b, out):
             )
 
         def h_turn(ct, half):
-            t1 = ps.tile([P, 4, P], F32, name="t1", tag="ps")
+            on_vector = (ct, half) in VECTOR_PIECES
+            t1 = ps.tile([P, 4, P], BF16 if on_vector else F32, name="t1", tag="ps")
             for a in range(4):
-                nc.tensor.matmul(
-                    out=t1[:, a, :],
-                    lhsT=h_sb[:, 4 * half + a, ct * P : (ct + 1) * P],
-                    rhs=ident_bf[:],
-                    start=True,
-                    stop=True,
-                )
+                piece = h_sb[:, 4 * half + a, ct * P : (ct + 1) * P]
+                if on_vector:
+                    nc.tensor.transpose(out=t1[:, a, :], in_=piece, identity=ident_bf[:])
+                else:
+                    nc.tensor.matmul(out=t1[:, a, :], lhsT=piece, rhs=ident_bf[:], start=True, stop=True)
             live["t1", ct, half] = t1
 
-        def h_affine(ct, half, vector=False):
+        def h_affine(ct, half):
             dst = hbt[:, ct, 512 * half : 512 * (half + 1)]
             src = live["t1", ct, half][:].rearrange("p a n -> p (a n)")
             gain = gb[:, ct : ct + 1]
             shift = gb[:, CT + ct : CT + ct + 1]
-            if vector:
+            if (ct, half) in VECTOR_PIECES:
                 nc.vector.tensor_scalar(out=dst, in0=src, scalar1=gain, scalar2=shift, op0=ALU.mult, op1=ALU.add)
             else:
                 nc.scalar.activation(out=dst, in_=src, func=ACT.Identity, scale=gain, bias=shift)
@@ -213,6 +213,15 @@ def tile_tls_msc_pb_kernel(tc, h, adj, gcn_bn_g, gcn_bn_b, gcn_w, gcn_b, out):
         def gn_turn(r):
             first = 2 * (r // 4)
             t3 = ps.tile([P, NU, P], F32, name="t3", tag="ps")
+            if r == 4:
+                for a in (4, 5):
+                    nc.tensor.matmul(
+                        out=t3[:].rearrange("p u i -> p (u i)"),
+                        lhsT=ident_bf[:],
+                        rhs=adj_sb[:, a, 512:N],
+                        start=True,
+                        stop=True,
+                    )
             words = gn[:, r, :].bitcast(F32)
             for u in range(first, NU):
                 nc.tensor.transpose(out=t3[:, u, :], in_=words[:, u * P : (u + 1) * P], identity=ident_f[:])
@@ -402,7 +411,7 @@ def tile_tls_msc_pb_kernel(tc, h, adj, gcn_bn_g, gcn_bn_b, gcn_w, gcn_b, out):
             scale(r, 2 * P, 4 * P)
         for ct in range(2, CT):
             h_turn(ct, 0)
-            h_affine(ct, 0, vector=(ct == 2))
+            h_affine(ct, 0)
         spread(2)
         spread(3)
         for ct in range(CT):
@@ -412,7 +421,7 @@ def tile_tls_msc_pb_kernel(tc, h, adj, gcn_bn_g, gcn_bn_b, gcn_w, gcn_b, out):
         w_group()
         for r in range(2):
             scale(r, 512, N)
-        h_affine(CT - 1, 1, vector=True)
+        h_affine(CT - 1, 1)
         for r in range(2, 4):
             scale(r, 512, N)
         for ct in range(CT):

from contextlib import ExitStack

from concourse import mybir
from concourse.masks import make_identity

BF16 = mybir.dt.bfloat16
F32 = mybir.dt.float32
U32 = mybir.dt.uint32
U8 = mybir.dt.uint8
FP8X4 = mybir.dt.float8_e4m3fn_x4
ALU = mybir.AluOpType
ACT = mybir.ActivationFunctionType

P = 128
N = 1024
D = 512
NT = N // P
CT = D // P
G = 2
NU = 4
T = 4
NEG_SLOPE = 0.01
VECTOR_PIECES = ((2, 0), (CT - 1, 1))
PAIR = (0, 1)

FLOPS = 2 * N * N * D + 2 * N * D * D


def tile_tls_msc_pb_kernel(tc, h, adj, gcn_bn_g, gcn_bn_b, gcn_w, gcn_b, out):
    nc = tc.nc
    with ExitStack() as ctx:
        keep = ctx.enter_context(tc.tile_pool(name="keep", bufs=1))
        eight = ctx.enter_context(tc.tile_pool(name="eight", bufs=NT))
        ps_c = ctx.enter_context(tc.psum_pool(name="ps_c", bufs=1))
        ps = ctx.enter_context(tc.psum_pool(name="ps", bufs=6))
        ctx.enter_context(tc.manual_schedule())

        ident_bf = keep.tile([P, P], BF16, name="ident_bf")
        ident_f = keep.tile([P, P], F32, name="ident_f")
        vecs = keep.tile([P, P], BF16, name="vecs")
        warm = keep.tile([P, 1], F32, name="warm")
        adj_sb = keep.tile([P, NT, N], BF16, name="adj_sb")
        h_sb = keep.tile([P, NT, D], BF16, name="h_sb")
        w_sb = keep.tile([P, T, D], BF16, name="w_sb")
        bias_bc = keep.tile([P, D], BF16, name="bias_bc")
        bias_hi = keep.tile([P, CT], F32, name="bias_hi")
        bias_lo = keep.tile([P, CT], F32, name="bias_lo")
        ag_pair_g = keep.tile([P, 2, P, T], BF16, name="ag_pair_g", align_bytes=64)
        ag_pair_q = keep.tile([P, 2 * P], U32, name="ag_pair_q", align_bytes=64)
        ag_pair_s = keep.tile([P, 2 * P], U8, name="ag_pair_s", align_bytes=64)
        hi = keep.tile([P, CT, 2 * P], F32, name="hi")
        low = keep.tile([P, CT, 2 * P], F32, name="low")
        ones = keep.tile([P, 1], BF16, name="ones")
        row_part = keep.tile([P, 4], F32, name="row_part")
        junk = keep.tile([P, N], BF16, name="junk")
        deg = keep.tile([P, NT], F32, name="deg")
        gd = keep.tile([P, NT, 2 * P], F32, name="gd")
        ident_2 = keep.tile([P, 2, P, 2], F32, name="ident_2")
        dinv = keep.tile([P, NT], F32, name="dinv")
        gb = keep.tile([P, 3 * CT], F32, name="gb")
        hbt = keep.tile([P, CT, N], BF16, name="hbt")
        hb_g = keep.tile([P, G, D, T], BF16, name="hb_g", align_bytes=64)
        hb_q = keep.tile([P, G, D], U32, name="hb_q", align_bytes=64)
        hb_s = keep.tile([P, G, D], U8, name="hb_s", align_bytes=64)
        w_g = keep.tile([P, D, T], BF16, name="w_g", align_bytes=64)
        w_q = keep.tile([P, D], U32, name="w_q", align_bytes=64)
        w_s = keep.tile([P, D], U8, name="w_s", align_bytes=64)
        gn = keep.tile([P, NT, N], BF16, name="gn")
        gn_q = keep.tile([P, NT, G, P], U32, name="gn_q", align_bytes=64)
        gn_s = keep.tile([P, NT, G, P], U8, name="gn_s", align_bytes=64)
        dbc = [ps_c.tile([P, 512], F32, name="dbc%d" % i) for i in range(2)]
        live = {}

        def setup():
            nc.vector.memset(vecs[:], 0.0)
            adj_v = adj.rearrange("(u p e) c -> u p e c", u=NU, e=2)
            h_v = h.rearrange("(a p) c -> p a c", p=P)
            for half in range(2):
                for u in range(2 * half, 2 * half + 2):
                    c = 512 * half
                    nc.sync.dma_start(out=adj_sb[:, 2 * u : 2 * u + 2, c:N], in_=adj_v[u, :, :, c:N])
                if half == 0:
                    for k, v in enumerate((gcn_bn_g, gcn_bn_b, gcn_b)):
                        nc.sync.dma_start(out=vecs[k * CT : (k + 1) * CT, :], in_=v.rearrange("(t p) -> t p", p=P))
                nc.sync.dma_start(out=h_sb[:, 4 * half : 4 * half + 4, :], in_=h_v[:, 4 * half : 4 * half + 4, :])
            nc.sync.dma_start(out=w_sb[:], in_=gcn_w.rearrange("(t p) d -> p t d", p=P))
            nc.sync.dma_start(out=bias_bc[:], in_=gcn_b.partition_broadcast(P))
            make_identity(nc, ident_bf[:])
            make_identity(nc, ident_f[:])
            nc.vector.memset(warm[:], 1.0)
            nc.vector.memset(ones[:], 1.0)
            nc.vector.memset(ident_2[:], 0.0)
            for e in range(2):
                nc.vector.tensor_copy(out=ident_2[:, e, :, e], in_=ident_f[:])
            nc.scalar.activation(out=warm[:], in_=warm[:], func=ACT.Abs_reciprocal_sqrt)

        def vec_columns():
            tv = ps.tile([P, P], BF16, name="tv", tag="ps")
            nc.tensor.transpose(out=tv[:], in_=vecs[:], identity=ident_bf[:])
            live["tv"] = tv

        def vec_copy():
            nc.scalar.copy(out=gb[:], in_=live["tv"][:, 0 : 3 * CT])

        def bias_columns():
            nc.scalar.activation(out=bias_hi[:], in_=gb[:, 2 * CT : 3 * CT], func=ACT.Copy, scale=1.0 - NEG_SLOPE)
            nc.scalar.activation(out=bias_lo[:], in_=gb[:, 2 * CT : 3 * CT], func=ACT.Copy, scale=NEG_SLOPE)

        def row_sum(r):
            right = adj_sb[:, r, 512 * (r // 2) : N]
            part = row_part[:, r : r + 1]
            if r % 2 == 0:
                nc.vector.tensor_reduce(out=part, in_=right, axis=mybir.AxisListType.X, op=ALU.add)
            else:
                nc.scalar.activation(out=junk[:, 512 * (r // 2) : N], in_=right, func=ACT.Copy, accum_out=part)

        def with_identity(r):
            u, e = divmod(r, 2)
            nc.gpsimd.tensor_tensor(
                out=gd[:, r, :],
                in0=adj_sb[:, r, 2 * P * u : 2 * P * (u + 1)],
                in1=ident_2[:, e, :, :].rearrange("p n e -> p (n e)"),
                op=ALU.add,
            )

        def column_sums(sums, rows, first):
            for k, r in enumerate(rows):
                u, e = divmod(r, 2)
                for a in range(first, first + 4):
                    nc.tensor.matmul(
                        out=sums[:, k : k + 1],
                        lhsT=adj_sb[:, a, 2 * P * u + e : 2 * P * (u + 1) : 2],
                        rhs=ones[:],
                        start=(a == first),
                        stop=(a == first + 3),
                    )

        def inv_roots(c, total):
            nc.scalar.activation(out=dinv[:, c], in_=total, func=ACT.Abs_reciprocal_sqrt, bias=1.0)

        def spread(u):
            for e in range(2):
                c = 2 * u + e
                nc.tensor.transpose(
                    out=roots[u][:, e : 2 * P : 2],
                    in_=dinv[:, c : c + 1].to_broadcast([P, P]),
                    identity=ident_f[:],
                )

        def scale(r, lo, hi):
            on_diagonal = (lo, hi) == (2 * P * (r // 2), 2 * P * (r // 2 + 1))
            nc.vector.scalar_tensor_tensor(
                out=gn[:, r, lo:hi],
                in0=gd[:, r, :] if on_diagonal else adj_sb[:, r, lo:hi],
                scalar=dinv[:, r : r + 1],
                in1=roots[lo // (2 * P)][:, 0 : hi - lo],
                op0=ALU.mult,
                op1=ALU.mult,
            )

        def h_turn(ct, half):
            on_vector = (ct, half) in VECTOR_PIECES
            t1 = ps.tile([P, 4, P], BF16 if on_vector else F32, name="t1", tag="ps")
            for a in range(4):
                piece = h_sb[:, 4 * half + a, ct * P : (ct + 1) * P]
                if on_vector:
                    nc.tensor.transpose(out=t1[:, a, :], in_=piece, identity=ident_bf[:])
                else:
                    nc.tensor.matmul(out=t1[:, a, :], lhsT=piece, rhs=ident_bf[:], start=True, stop=True)
            live["t1", ct, half] = t1

        def h_affine(ct, half):
            dst = hbt[:, ct, 512 * half : 512 * (half + 1)]
            src = live["t1", ct, half][:].rearrange("p a n -> p (a n)")
            gain = gb[:, ct : ct + 1]
            shift = gb[:, CT + ct : CT + ct + 1]
            if (ct, half) in VECTOR_PIECES:
                nc.vector.tensor_scalar(out=dst, in0=src, scalar1=gain, scalar2=shift, op0=ALU.mult, op1=ALU.add)
            else:
                nc.scalar.activation(out=dst, in_=src, func=ACT.Identity, scale=gain, bias=shift)

        def hb_turn(ct):
            t2 = ps.tile([P, NU, P], F32, name="t2", tag="ps")
            words = hbt[:, ct, :].bitcast(F32)
            for u in range(NU):
                nc.tensor.transpose(out=t2[:, u, :], in_=words[:, u * P : (u + 1) * P], identity=ident_f[:])
            live["t2", ct] = t2

        def hb_group(ct):
            words = hb_g[:].rearrange("p g c t -> p (g c t)").bitcast(F32).rearrange("p (g c u) -> p g c u", g=G, u=2)
            nc.scalar.copy(
                out=words[:, :, ct * P : (ct + 1) * P, :],
                in_=live["t2", ct][:].rearrange("p (g u) c -> p g c u", g=G),
            )

        def hb_quant(g):
            nc.vector.quantize_mx(
                out=hb_q[:, g, :].bitcast(FP8X4),
                scales=hb_s[:, g, :],
                in_=hb_g[:, g, :, :].rearrange("p c t -> p (c t)"),
            )

        def w_group():
            nc.gpsimd.tensor_scalar(
                out=w_g[:], in0=w_sb[:].rearrange("p t d -> p d t"), scalar1=1.0, scalar2=0.0, op0=ALU.mult, op1=ALU.add
            )

        def w_quant():
            nc.vector.quantize_mx(
                out=w_q[:].bitcast(FP8X4), scales=w_s[:], in_=w_g[:].rearrange("p d t -> p (d t)")
            )

        def gn_turn(r):
            first = 2 * (r // 4)
            t3 = ps.tile([P, NU, P], F32, name="t3", tag="ps")
            if r == 4:
                for a in (4, 5):
                    nc.tensor.matmul(
                        out=t3[:].rearrange("p u i -> p (u i)"),
                        lhsT=ident_bf[:],
                        rhs=adj_sb[:, a, 512:N],
                        start=True,
                        stop=True,
                    )
            words = gn[:, r, :].bitcast(F32)
            for u in range(first, NU):
                nc.tensor.transpose(out=t3[:, u, :], in_=words[:, u * P : (u + 1) * P], identity=ident_f[:])
            live["t3", r] = t3

        def gn_group(r):
            gn_g = live["gn_g", r]
            first = r // 4
            words = gn_g[:].rearrange("p g i t -> p (g i t)").bitcast(F32).rearrange("p (g i u) -> p g i u", g=G, u=2)
            nc.scalar.copy(
                out=words[:, first:G, :, :],
                in_=live["t3", r][:, 2 * first : NU, :].rearrange("p (g u) i -> p g i u", u=2),
            )

        def gn_tile(r):
            gn_g = eight.tile([P, G, P, T], BF16, name="gn_g", align_bytes=64)
            live["gn_g", r] = gn_g
            if r >= 4:
                group, e = divmod(r, 2)
                nc.gpsimd.tensor_scalar(
                    out=gn_g[:, 0, :, :],
                    in0=gn[:, 0:4, 2 * P * group + e : 2 * P * (group + 1) : 2].rearrange("p t i -> p i t"),
                    scalar1=1.0,
                    scalar2=0.0,
                    op0=ALU.mult,
                    op1=ALU.add,
                )

        def gn_quant(b):
            nc.vector.quantize_mx(
                out=gn_q[:, b, :, :].rearrange("p g i -> p (g i)").bitcast(FP8X4),
                scales=gn_s[:, b, :, :].rearrange("p g i -> p (g i)"),
                in_=live["gn_g", b][:].rearrange("p g i t -> p (g i t)"),
            )

        def first_matmul(b):
            m1 = ps.tile([P, CT, P], F32, name="m1", tag="ps")
            for ct in range(CT):
                for g in range(G):
                    nc.tensor.matmul_mx(
                        out=m1[:, ct, :],
                        lhsT=hb_q[:, g, ct * P : (ct + 1) * P].bitcast(FP8X4),
                        lhsT_scale=hb_s[:, g, ct * P : (ct + 1) * P],
                        rhs=gn_q[:, b, g, :].bitcast(FP8X4),
                        rhs_scale=gn_s[:, b, g, :],
                        start=(g == 0),
                        stop=(g == G - 1),
                    )
            live["m1", b] = m1

        def agg_group(b):
            if b in PAIR:
                ag_g = ag_pair_g[:, b, :, :]
            else:
                ag_g = eight.tile([P, P, T], BF16, name="ag_g", align_bytes=64)[:]
            nc.scalar.copy(out=ag_g, in_=live["m1", b][:].rearrange("p t i -> p i t"))
            live["ag_g", b] = ag_g

        def agg_quant(b):
            ag_q = eight.tile([P, P], U32, name="ag_q", align_bytes=64)
            ag_s = eight.tile([P, P], U8, name="ag_s", align_bytes=64)
            nc.vector.quantize_mx(
                out=ag_q[:].bitcast(FP8X4), scales=ag_s[:], in_=live["ag_g", b].rearrange("p i t -> p (i t)")
            )
            live["ag_q", b] = (ag_q, ag_s)

        def second_matmul(b):
            ag_q, ag_s = live["ag_q", b]
            m2 = ps_c.tile([P, D], F32, name="m2", tag="dbc%d" % (b % 2))
            nc.tensor.matmul_mx(
                out=m2[:],
                lhsT=ag_q[:].bitcast(FP8X4),
                lhsT_scale=ag_s[:],
                rhs=w_q[:].bitcast(FP8X4),
                rhs_scale=w_s[:],
                start=True,
                stop=True,
            )
            live["m2", b] = m2

        def pair_quant():
            nc.vector.quantize_mx(
                out=ag_pair_q[:].bitcast(FP8X4),
                scales=ag_pair_s[:],
                in_=ag_pair_g[:].rearrange("p b i t -> p (b i t)"),
            )

        def pair_matmul():
            for j in range(2):
                m2 = ps.tile([P, 2, 2 * P], F32, name="m2t", tag="ps")
                for c in range(2):
                    ct = 2 * j + c
                    nc.tensor.matmul_mx(
                        out=m2[:, c, :],
                        lhsT=w_q[:, ct * P : (ct + 1) * P].bitcast(FP8X4),
                        lhsT_scale=w_s[:, ct * P : (ct + 1) * P],
                        rhs=ag_pair_q[:].bitcast(FP8X4),
                        rhs_scale=ag_pair_s[:],
                        start=True,
                        stop=True,
                    )
                live["m2t", j] = m2

        def pair_leaky(j):
            for c in range(2):
                ct = 2 * j + c
                src = live["m2t", j][:, c, :]
                nc.scalar.activation(
                    out=hi[:, ct, :], in_=src, func=ACT.Relu, scale=1.0 - NEG_SLOPE, bias=bias_hi[:, ct : ct + 1]
                )
                nc.scalar.activation(
                    out=low[:, ct, :], in_=src, func=ACT.Identity, scale=NEG_SLOPE, bias=bias_lo[:, ct : ct + 1]
                )

        def pair_turn(h):
            n = ps.tile([P, CT, P], F32, name="n", tag="ps")
            for ct in range(CT):
                for part, first in ((hi, True), (low, False)):
                    nc.tensor.matmul(
                        out=n[:, ct, :],
                        lhsT=part[:, ct, h * P : (h + 1) * P],
                        rhs=ident_f[:],
                        is_transpose=True,
                        start=first,
                        stop=not first,
                    )
            live["n", h] = n

        def pair_store(h):
            res = eight.tile([P, D], F32, name="res")
            nc.scalar.copy(out=res[:], in_=live["n", h][:].rearrange("p c d -> p (c d)"))
            store(h, res)

        def store(b, res):
            out_v = out.rearrange("(u p e) d -> u e p d", u=NU, e=2)
            nc.sync.dma_start(out=out_v[b // 2, b % 2], in_=res[:])

        def add_bias(b):
            lin = eight.tile([P, D], F32, name="lin")
            nc.vector.tensor_tensor(out=lin[:], in0=live["m2", b][:], in1=bias_bc[:], op=ALU.add)
            live["lin", b] = lin

        def leaky(b):
            lin = live["lin", b]
            res = eight.tile([P, D], F32, name="res")
            nc.vector.scalar_tensor_tensor(
                out=res[:], in0=lin[:], scalar=NEG_SLOPE, in1=lin[:], op0=ALU.mult, op1=ALU.max
            )
            store(b, res)

        setup()
        first_roots = ps.tile([P, 2 * P], F32, name="first_roots", tag="ps")
        roots = [first_roots[:], dbc[0][:, 0 : 2 * P], dbc[1][:], dbc[1][:, 2 * P : 4 * P]]
        sums_1 = ps.tile([P, 2], F32, name="sums_1", tag="ps")
        sums_2 = ps.tile([P, 2, 4], F32, name="sums_2", tag="ps")
        for r in range(NT):
            with_identity(r)
        for r in range(4):
            gn_tile(r)
        row_sum(0)
        row_sum(1)
        inv_roots(slice(0, 2), row_part[:, 0:2])
        row_sum(2)
        row_sum(3)
        column_sums(sums_1[:], (2, 3), 0)
        nc.vector.tensor_tensor(out=deg[:, 2:4], in0=sums_1[:], in1=row_part[:, 2:4], op=ALU.add)
        inv_roots(slice(2, 4), deg[:, 2:4])
        spread(0)
        column_sums(sums_2[:, 0, :], range(4, NT), 0)
        vec_columns()
        vec_copy()
        h_turn(0, 0)
        h_affine(0, 0)
        for r in range(4):
            scale(r, 0, 2 * P)
        spread(1)
        h_turn(1, 0)
        h_affine(1, 0)
        for r in range(2):
            scale(r, 2 * P, 4 * P)
        column_sums(sums_2[:, 1, :], range(4, NT), 4)
        nc.vector.tensor_reduce(
            out=deg[:, 4:8], in_=sums_2[:].rearrange("p k r -> p r k"), axis=mybir.AxisListType.X, op=ALU.add
        )
        inv_roots(slice(4, 8), deg[:, 4:8])
        for r in range(2, 4):
            scale(r, 2 * P, 4 * P)
        for ct in range(2, CT):
            h_turn(ct, 0)
            h_affine(ct, 0)
        spread(2)
        spread(3)
        for ct in range(CT):
            h_turn(ct, 1)
        for ct in range(CT - 1):
            h_affine(ct, 1)
        w_group()
        for r in range(2):
            scale(r, 512, N)
        h_affine(CT - 1, 1)
        for r in range(2, 4):
            scale(r, 512, N)
        for ct in range(CT):
            hb_turn(ct)
            hb_group(ct)
        for r in range(4, NT):
            gn_tile(r)
            scale(r, 512, 512 + 2 * P)
            scale(r, 512 + 2 * P, N)
        hb_quant(0)
        hb_quant(1)
        for r in range(NT):
            gn_turn(r)
            gn_group(r)
        bias_columns()
        for r in range(5):
            gn_quant(r)
            first_matmul(r)
        gn_quant(5)
        w_quant()
        agg_group(0)
        agg_group(1)
        pair_quant()
        pair_matmul()
        for k in range(2, NT + 2):
            if k < NT:
                agg_group(k)
                agg_quant(k)
                second_matmul(k)
            if k + 3 < NT:
                first_matmul(k + 3)
            if k == 2:
                gn_quant(6)
                gn_quant(7)
            if k in (4, 5):
                pair_leaky(k - 4)
            if k == 6:
                pair_turn(0)
                pair_turn(1)
            if k in (7, 8):
                pair_store(k - 7)
            if 2 <= k - 1 < NT:
                add_bias(k - 1)
            if k >= 4:
                leaky(k - 2)
